import numpy as np
import ml_dtypes


def mxq(x, axis, fmt="e4m3"):
    dtype, down = {"e4m3": (ml_dtypes.float8_e4m3fn, 7), "e5m2": (ml_dtypes.float8_e5m2, 14)}[fmt]
    v = np.moveaxis(np.asarray(x, np.float32).astype(ml_dtypes.bfloat16).astype(np.float64), axis, -1)
    blocks = v.reshape(v.shape[:-1] + (-1, 32))
    amax = np.abs(blocks).max(-1, keepdims=True)
    byte = np.maximum(np.where(amax > 0, np.frexp(amax)[1] - 1 + 127, 0) - down, 1)
    scale = np.exp2(byte - 127.0)
    codes = (blocks / scale).astype(np.float32).astype(dtype).astype(np.float64)
    return np.moveaxis((codes * scale).reshape(v.shape), -1, axis)


WIDE = False


def mx_kscale(k):
    if not WIDE:
        return np.ones(k)
    levels = np.array([10, -10, 5, -5, 0])
    a = np.random.permutation(np.resize(levels, k // 512 * 4)).reshape(k // 512, 4)
    idx = np.arange(k)
    return np.exp2(a[idx // 512, idx % 128 // 32])


BF16 = ml_dtypes.bfloat16


def bf(x):
    return np.asarray(x, np.float32).astype(BF16)


def f64(x):
    return np.asarray(x).astype(np.float64)


E2M1 = np.array([0.0, 0.5, 1.0, 1.5, 2.0, 3.0, 4.0, 6.0, -0.0, -0.5, -1.0, -1.5, -2.0, -3.0, -4.0, -6.0])


def pack_weight(w, fmt):
    k, n = w.shape
    w = f64(bf(w)).reshape(k // 32, 32, n)
    amax = np.abs(w).max(1)
    if fmt == "e4m3":
        byte = np.frexp(amax)[1] - 1 + 127 - 7
    else:
        mant, ex = np.frexp(amax / 6.0)
        byte = np.where(mant > 0.5, ex, ex - 1) + 127
    byte = np.clip(np.where(amax > 0, byte, 1), 1, 254)
    scaled = (w * np.exp2(127.0 - byte)[:, None, :]).reshape(k, n).astype(np.float32)
    by_word = np.ascontiguousarray(scaled.reshape(k // 512, 128, 4, n).transpose(0, 1, 3, 2))
    if fmt == "e4m3":
        words = by_word.astype(ml_dtypes.float8_e4m3fn).view(np.uint8)
    else:
        c = by_word.astype(ml_dtypes.float4_e2m1fn).view(np.uint8) & 0xF
        words = c[..., 0::2] | (c[..., 1::2] << 4)
    return np.ascontiguousarray(words), np.ascontiguousarray(byte.astype(np.uint8).reshape(k // 512, 16, n))


def unpack_weight(words, scales, fmt):
    g, p, n, _ = words.shape
    if fmt == "e4m3":
        vals = np.ascontiguousarray(words).view(ml_dtypes.float8_e4m3fn).astype(np.float64)
    else:
        nib = np.empty((g, p, n, 4), np.uint8)
        nib[..., 0::2] = words & 0xF
        nib[..., 1::2] = words >> 4
        vals = E2M1[nib]
    vals = vals * np.repeat(np.exp2(scales.astype(np.float64) - 127.0), 8, axis=1)[..., None]
    return vals.transpose(0, 1, 3, 2).reshape(g * 512, n)


M, B, I, H, O = 5, 896, 128, 1024, 64
O2 = 2 * O
EPS = 1e-6


def softplus(v):
    return np.maximum(v, 0.0) + np.log(1.0 + np.exp(-np.abs(v)))


def setup_inputs():
    s, t = mx_kscale(H), mx_kscale(H)
    h1 = bf(np.maximum(np.random.standard_normal((M, B, H)), 0.0) * s)
    W2 = np.random.standard_normal((M, H, H)) * 1.4 / np.sqrt(H) * t[None, :, None] / s[None, None, :]
    W2_words, W2_scales = pack_weight(W2.swapaxes(1, 2).reshape(-1, H), "e4m3")
    b2 = bf(np.random.standard_normal((M, H)) * 0.3 * t)
    W3 = np.random.standard_normal((M, O2, H)) * 1.4 / np.sqrt(H) / t[None, None, :]
    W3_words, W3_scales = pack_weight(W3.swapaxes(1, 2).reshape(-1, O2), "e4m3")
    b3 = bf(np.random.standard_normal((M, O2)) * 0.3)
    return {"h1": h1,
            "W2_words": W2_words, "W2_scales": W2_scales,
            "b2": b2,
            "W3_words": W3_words, "W3_scales": W3_scales,
            "b3": b3}


def reference(h1, W2_words, W2_scales, b2, W3_words, W3_scales, b3):
    h2 = np.maximum((mxq(f64(h1), 2, "e4m3") @ unpack_weight(W2_words, W2_scales, "e4m3").reshape(M, H, H)) + f64(b2)[:, None, :], 0.0)
    y = (mxq(h2, 2, "e4m3") @ unpack_weight(W3_words, W3_scales, "e4m3").reshape(M, H, O2)) + f64(b3)[:, None, :]
    means = y[:, :, :O]
    variances = softplus(y[:, :, O:]) + EPS
    mean = means.mean(axis=0)
    variance = (variances + means ** 2).mean(axis=0) - mean ** 2
    variance = np.maximum(variance, 0.0) + EPS
    return mean, variance

@@ -1,0 +1,316 @@
+from contextlib import ExitStack
+
+import concourse.mybir as mybir
+from concourse.masks import make_identity
+
+F32 = mybir.dt.float32
+BF16 = mybir.dt.bfloat16
+I32 = mybir.dt.int32
+U32 = mybir.dt.uint32
+U8 = mybir.dt.uint8
+FP8X4 = mybir.dt.float8_e4m3fn_x4
+ALU = mybir.AluOpType
+ACT = mybir.ActivationFunctionType
+
+MODELS = 5
+BATCH = 896
+HIDDEN = 1024
+OUT2 = 128
+OUT = OUT2 // 2
+EPS = 1e-6
+
+P = 128
+PACK = 4
+K_PASS = P * PACK
+PASSES = HIDDEN // K_PASS
+TILES = BATCH // P
+BANK = 512
+HALVES = HIDDEN // BANK
+PLANES = 4
+
+ROUND = 2
+H1_LEAD = 3
+
+FLOPS = 2 * MODELS * BATCH * HIDDEN * (HIDDEN + OUT2)
+
+
+def rounds_of_row_tiles():
+    rounds = []
+    for m in range(MODELS):
+        for first in range(0, TILES, ROUND):
+            rounds.append((m, first, min(ROUND, TILES - first)))
+    return rounds
+
+
+def tile_gaussianmixturemlp_pa_t_e_kernel(
+    tc, h1, W2_words, W2_scales, b2, W3_words, W3_scales, b3, out_0, out_1
+):
+    nc = tc.nc
+    rounds = rounds_of_row_tiles()
+    all_passes = MODELS * PASSES
+
+    with ExitStack() as ctx:
+        keep = ctx.enter_context(tc.tile_pool(name="keep", bufs=1))
+        stage = ctx.enter_context(tc.tile_pool(name="stage", bufs=2))
+        psum_flip = ctx.enter_context(tc.psum_pool(name="psum_flip", bufs=4))
+        psum_h2 = ctx.enter_context(tc.psum_pool(name="psum_h2", bufs=3))
+        psum_y = ctx.enter_context(tc.psum_pool(name="psum_y", bufs=1))
+        ctx.enter_context(tc.manual_schedule())
+
+        h1_sb = [keep.tile([P, TILES, HIDDEN], BF16, name="h1_sb%d" % m) for m in range(MODELS)]
+        w2_words = keep.tile([P, all_passes, PACK * HIDDEN], U8, align_bytes=64)
+        w3_words = keep.tile([P, all_passes, PACK * OUT2], U8, align_bytes=64)
+        w2_planes = keep.tile([P, (all_passes + PLANES - 1) // PLANES, HIDDEN], U8, align_bytes=64)
+        w3_planes = keep.tile([P, all_passes, OUT2], U8, align_bytes=64)
+        b2_rows = keep.tile([P, HIDDEN], BF16)
+        b2_all = keep.tile([P, MODELS, HIDDEN], BF16)
+        b3_all = keep.tile([P, MODELS, OUT2], BF16)
+        ident = keep.tile([P, P], F32)
+        ident_bf = keep.tile([P, P], BF16)
+        mean_sum = keep.tile([P, TILES, OUT], F32)
+        var_sum = keep.tile([P, TILES, OUT], F32)
+        factors = keep.tile([P, TILES, OUT], F32)
+
+        nc.vector.memset(w2_planes[:].bitcast(I32), 0)
+        nc.vector.memset(w3_planes[:].bitcast(I32), 0)
+        nc.vector.memset(b2_rows[:], 0.0)
+        nc.vector.memset(mean_sum[:], 0.0)
+        nc.vector.memset(var_sum[:], MODELS * EPS)
+        nc.vector.memset(factors[:], 1.0)
+        make_identity(nc, ident[:])
+        nc.vector.tensor_copy(out=ident_bf[:], in_=ident[:])
+
+        def load_h1(m, first, count):
+            rows = h1[m].rearrange("(p i) k -> p i k", i=TILES)
+            nc.sync.dma_start(
+                out=h1_sb[m][:, first : first + count, :], in_=rows[:, first : first + count, :]
+            )
+
+        def load_w2(m):
+            c0 = PASSES * m
+            nc.sync.dma_start(
+                out=w2_words[:, c0 : c0 + PASSES, :].bitcast(I32),
+                in_=W2_words[c0 : c0 + PASSES].rearrange("g p n t -> p g (n t)").bitcast(I32),
+            )
+
+        load_h1(0, 0, ROUND)
+        nc.sync.dma_start(out=b2_rows[0:MODELS, :], in_=b2)
+        w2_planes_i32 = w2_planes[:].bitcast(I32)
+        for c0 in range(0, all_passes, PLANES):
+            n_planes = min(PLANES, all_passes - c0)
+            for quadrant in range(4):
+                nc.sync.dma_start(
+                    out=w2_planes_i32[32 * quadrant : 32 * quadrant + 4 * n_planes, c0 // PLANES, :],
+                    in_=W2_scales[c0 : c0 + n_planes, 4 * quadrant : 4 * quadrant + 4, :].bitcast(I32),
+                )
+        w3_planes_i32 = w3_planes[:].bitcast(I32)
+        for quadrant in range(4):
+            nc.sync.dma_start(
+                out=w3_planes_i32[32 * quadrant : 32 * quadrant + 4, :, :],
+                in_=W3_scales[:, 4 * quadrant : 4 * quadrant + 4, :]
+                .rearrange("c r n -> r c n")
+                .bitcast(I32),
+            )
+        load_h1(0, ROUND, TILES - ROUND)
+        load_w2(0)
+        nc.sync.dma_start(
+            out=w3_words[:].bitcast(I32),
+            in_=W3_words.rearrange("g p n t -> p g (n t)").bitcast(I32),
+        )
+        nc.sync.dma_start(
+            out=b3_all[:].rearrange("p m o -> p (m o)"),
+            in_=b3.rearrange("m o -> (m o)").partition_broadcast(P),
+        )
+        for m in range(1, MODELS):
+            load_h1(m, 0, TILES)
+            load_w2(m)
+
+        def sorted_view(columns):
+            return columns.rearrange("b (p u e) -> b u p e", u=2, e=2)
+
+        for m in range(MODELS):
+            for half in range(HALVES):
+                spread = psum_h2.tile([P, BANK], F32, tag="h2_bank")
+                nc.tensor.matmul(
+                    out=spread[:],
+                    lhsT=ident_bf[:, m : m + 1].to_broadcast([P, P]),
+                    rhs=b2_rows[:, BANK * half : BANK * (half + 1)],
+                    start=True,
+                    stop=True,
+                )
+                nc.vector.tensor_copy(
+                    out=b2_all[:, m, BANK * half : BANK * (half + 1)].rearrange(
+                        "b (u p e) -> b u p e", u=2, e=2
+                    ),
+                    in_=sorted_view(spread[:]),
+                )
+
+        held = {}
+
+        def transpose_h1(r):
+            m, first, count = rounds[r]
+            words = h1_sb[m][:].bitcast(F32)
+            grouped = stage.tile([P, ROUND, PASSES, P, PACK], BF16, tag="h1_grouped", align_bytes=64)
+            for j in range(count):
+                flipped = psum_flip.tile([P, PASSES * 2, P], F32, tag="flipped")
+                for g in range(PASSES):
+                    for u in range(2):
+                        nc.tensor.transpose(
+                            flipped[:, 2 * g + u, :],
+                            words[:, first + j, 256 * g + u : 256 * (g + 1) : 2],
+                            ident[:],
+                        )
+                nc.scalar.copy(
+                    out=grouped[:, j].bitcast(F32),
+                    in_=flipped[:].rearrange("p (g u) b -> p g b u", u=2),
+                )
+            held["h1_grouped", r] = grouped
+
+        def quantise(r, what, bufs):
+            count = rounds[r][2]
+            grouped = held[what + "_grouped", r]
+            codes = stage.tile([P, ROUND, PASSES, P], U32, tag=what + "_codes", bufs=bufs, align_bytes=64)
+            scales = stage.tile([P, ROUND, PASSES, P], U8, tag=what + "_scales", bufs=bufs, align_bytes=64)
+            nc.vector.quantize_mx(
+                out=codes[:, 0:count].rearrange("p j g b -> p (j g b)").bitcast(FP8X4),
+                scales=scales[:, 0:count].rearrange("p j g b -> p (j g b)"),
+                in_=grouped[:, 0:count].rearrange("p j g b t -> p (j g b t)"),
+            )
+            held[what + "_mx", r] = (codes, scales)
+
+        def layer2(r):
+            m, first, count = rounds[r]
+            codes, scales = held["h1_mx", r]
+            h2 = stage.tile([P, ROUND, HALVES, BANK], BF16, tag="h2")
+            for j in range(count):
+                for half in range(HALVES):
+                    bank = psum_h2.tile([P, BANK], F32, tag="h2_bank")
+                    for g in range(PASSES):
+                        c = PASSES * m + g
+                        nc.tensor.matmul_mx(
+                            out=bank[:],
+                            lhsT=codes[:, j, g, :].bitcast(FP8X4),
+                            lhsT_scale=scales[:, j, g, :],
+                            rhs=w2_words[:, c, PACK * BANK * half : PACK * BANK * (half + 1)].bitcast(FP8X4),
+                            rhs_scale=w2_planes[
+                                4 * (c % PLANES) : P, c // PLANES, BANK * half : BANK * (half + 1)
+                            ],
+                            start=(g == 0),
+                            stop=(g == PASSES - 1),
+                        )
+                    nc.vector.tensor_tensor(
+                        out=h2[:, j, half, :].rearrange("b (u p e) -> b u p e", u=2, e=2),
+                        in0=sorted_view(bank[:]),
+                        in1=b2_all[:, m, BANK * half : BANK * (half + 1)].rearrange(
+                            "b (u p e) -> b u p e", u=2, e=2
+                        ),
+                        op=ALU.add,
+                    )
+            held["h2", r] = h2
+
+        def transpose_h2(r):
+            count = rounds[r][2]
+            h2 = held["h2", r]
+            grouped = stage.tile([P, ROUND, PASSES, P, PACK], BF16, tag="h2_grouped", align_bytes=64)
+            for j in range(count):
+                words = h2[:, j].rearrange("b g n -> b (g n)").bitcast(F32)
+                flipped = psum_flip.tile([P, PASSES * 2, P], F32, tag="flipped")
+                for gu in range(PASSES * 2):
+                    nc.tensor.transpose(flipped[:, gu, :], words[:, P * gu : P * (gu + 1)], ident[:])
+                pairs = flipped[:].bitcast(BF16)
+                for g in range(PASSES):
+                    nc.scalar.activation(
+                        out=grouped[:, j, g].rearrange("p b (u e) -> p b u e", e=2),
+                        in_=pairs[:, 2 * g : 2 * g + 2, :].rearrange("p u (b e) -> p b u e", e=2),
+                        func=ACT.Relu,
+                    )
+            held["h2_grouped", r] = grouped
+
+        def layer3(r):
+            m, first, count = rounds[r]
+            codes, scales = held["h2_mx", r]
+            if first == 0:
+                y_new = stage.tile([P, TILES, OUT2], F32, tag="y")
+                held["y", m] = y_new
+            y = held["y", m]
+            y_bank = psum_y.tile([P, ROUND, OUT2], F32, tag="y_bank")
+            for j in range(count):
+                for g in range(PASSES):
+                    c = PASSES * m + g
+                    nc.tensor.matmul_mx(
+                        out=y_bank[:, j, :],
+                        lhsT=codes[:, j, g, :].bitcast(FP8X4),
+                        lhsT_scale=scales[:, j, g, :],
+                        rhs=w3_words[:, c, :].bitcast(FP8X4),
+                        rhs_scale=w3_planes[:, c, :],
+                        start=(g == 0),
+                        stop=(g == PASSES - 1),
+                    )
+            nc.vector.tensor_tensor(
+                out=y[:, first : first + count, :],
+                in0=y_bank[:, 0:count, :],
+                in1=b3_all[:, m, :].unsqueeze(1).to_broadcast([P, count, OUT2]),
+                op=ALU.add,
+            )
+
+        def closes_model(r):
+            return rounds[r][1] + rounds[r][2] == TILES
+
+        def head_functions(r):
+            if not closes_model(r):
+                return
+            y = held["y", rounds[r][0]]
+            size = stage.tile([P, TILES, OUT], F32, tag="size")
+            decay = stage.tile([P, TILES, OUT], F32, tag="decay")
+            square = stage.tile([P, TILES, OUT], F32, tag="square")
+            nc.scalar.activation(out=size[:], in_=y[:, :, OUT:OUT2], func=ACT.Abs)
+            nc.scalar.activation(out=decay[:], in_=size[:], func=ACT.Exp, scale=-1.0)
+            nc.scalar.activation(out=square[:], in_=y[:, :, 0:OUT], func=ACT.Square)
+            held["decay", r] = decay
+            held["square", r] = square
+
+        def head_sums(r):
+            if not closes_model(r):
+                return
+            y = held["y", rounds[r][0]]
+            decay = held["decay", r]
+            square = held["square", r]
+            nc.gpsimd.tensor_tensor(out=mean_sum[:], in0=mean_sum[:], in1=y[:, :, 0:OUT], op=ALU.add)
+            nc.vector.scalar_tensor_tensor(
+                out=var_sum[:], in0=y[:, :, OUT:OUT2], scalar=0.0, in1=var_sum[:], op0=ALU.max, op1=ALU.add
+            )
+            nc.vector.scalar_tensor_tensor(
+                out=factors[:], in0=decay[:], scalar=1.0, in1=factors[:], op0=ALU.add, op1=ALU.mult
+            )
+            nc.vector.tensor_tensor(out=var_sum[:], in0=var_sum[:], in1=square[:], op=ALU.add)
+
+        def step(stage_of_round, r):
+            if 0 <= r < len(rounds):
+                stage_of_round(r)
+
+        for s in range(len(rounds) + H1_LEAD + 4):
+            step(lambda r: quantise(r, "h1", H1_LEAD + 1), s - 1)
+            step(lambda r: quantise(r, "h2", 2), s - H1_LEAD - 2)
+            step(head_sums, s - H1_LEAD - 4)
+            step(transpose_h1, s)
+            step(transpose_h2, s - H1_LEAD - 1)
+            step(layer2, s - H1_LEAD)
+            step(layer3, s - H1_LEAD - 2)
+            step(head_functions, s - H1_LEAD - 3)
+
+        log_sum = keep.tile([P, TILES, OUT], F32)
+        mean = keep.tile([P, TILES, OUT], F32)
+        mean_sq = keep.tile([P, TILES, OUT], F32)
+        variance = keep.tile([P, TILES, OUT], F32)
+        nc.scalar.activation(out=log_sum[:], in_=factors[:], func=ACT.Ln)
+        nc.vector.tensor_scalar_mul(out=mean[:], in0=mean_sum[:], scalar1=1.0 / MODELS)
+        nc.sync.dma_start(out=out_0.rearrange("(p i) o -> p i o", i=TILES), in_=mean[:])
+        nc.vector.tensor_tensor(out=mean_sq[:], in0=mean[:], in1=mean[:], op=ALU.mult)
+        nc.vector.tensor_tensor(out=var_sum[:], in0=var_sum[:], in1=log_sum[:], op=ALU.add)
+        nc.vector.scalar_tensor_tensor(
+            out=variance[:], in0=var_sum[:], scalar=1.0 / MODELS, in1=mean_sq[:], op0=ALU.mult, op1=ALU.subtract
+        )
+        nc.vector.tensor_scalar(
+            out=variance[:], in0=variance[:], scalar1=0.0, scalar2=EPS, op0=ALU.max, op1=ALU.add
+        )
+        nc.sync.dma_start(out=out_1.rearrange("(p i) o -> p i o", i=TILES), in_=variance[:])

@@ -29,6 +29,7 @@ HALVES = HIDDEN // BANK
 PLANES = 4
 
 ROUND = 2
+WHOLE_ROUNDS = TILES - TILES % ROUND
 H1_LEAD = 3
 
 FLOPS = 2 * MODELS * BATCH * HIDDEN * (HIDDEN + OUT2)
@@ -52,8 +53,8 @@ def tile_gaussianmixturemlp_pa_t_e_kernel(
     with ExitStack() as ctx:
         keep = ctx.enter_context(tc.tile_pool(name="keep", bufs=1))
         stage = ctx.enter_context(tc.tile_pool(name="stage", bufs=2))
-        psum_flip = ctx.enter_context(tc.psum_pool(name="psum_flip", bufs=4))
-        psum_h2 = ctx.enter_context(tc.psum_pool(name="psum_h2", bufs=3))
+        psum_flip = ctx.enter_context(tc.psum_pool(name="psum_flip", bufs=3))
+        psum_h2 = ctx.enter_context(tc.psum_pool(name="psum_h2", bufs=4))
         psum_y = ctx.enter_context(tc.psum_pool(name="psum_y", bufs=1))
         ctx.enter_context(tc.manual_schedule())
 
@@ -93,16 +94,21 @@ def tile_gaussianmixturemlp_pa_t_e_kernel(
                 in_=W2_words[c0 : c0 + PASSES].rearrange("g p n t -> p g (n t)").bitcast(I32),
             )
 
-        load_h1(0, 0, ROUND)
-        nc.sync.dma_start(out=b2_rows[0:MODELS, :], in_=b2)
-        w2_planes_i32 = w2_planes[:].bitcast(I32)
-        for c0 in range(0, all_passes, PLANES):
+        def load_w2_planes(c0):
             n_planes = min(PLANES, all_passes - c0)
             for quadrant in range(4):
                 nc.sync.dma_start(
-                    out=w2_planes_i32[32 * quadrant : 32 * quadrant + 4 * n_planes, c0 // PLANES, :],
+                    out=w2_planes[:].bitcast(I32)[
+                        32 * quadrant : 32 * quadrant + 4 * n_planes, c0 // PLANES, :
+                    ],
                     in_=W2_scales[c0 : c0 + n_planes, 4 * quadrant : 4 * quadrant + 4, :].bitcast(I32),
                 )
+
+        load_h1(0, 0, ROUND)
+        nc.sync.dma_start(out=b2_rows[0:MODELS, :], in_=b2)
+        load_w2_planes(0)
+        load_h1(0, ROUND, TILES - ROUND)
+        load_w2(0)
         w3_planes_i32 = w3_planes[:].bitcast(I32)
         for quadrant in range(4):
             nc.sync.dma_start(
@@ -111,8 +117,6 @@ def tile_gaussianmixturemlp_pa_t_e_kernel(
                 .rearrange("c r n -> r c n")
                 .bitcast(I32),
             )
-        load_h1(0, ROUND, TILES - ROUND)
-        load_w2(0)
         nc.sync.dma_start(
             out=w3_words[:].bitcast(I32),
             in_=W3_words.rearrange("g p n t -> p g (n t)").bitcast(I32),
@@ -122,6 +126,8 @@ def tile_gaussianmixturemlp_pa_t_e_kernel(
             in_=b3.rearrange("m o -> (m o)").partition_broadcast(P),
         )
         for m in range(1, MODELS):
+            if (PASSES * m) % PLANES == 0:
+                load_w2_planes(PASSES * m)
             load_h1(m, 0, TILES)
             load_w2(m)
 
@@ -138,7 +144,7 @@ def tile_gaussianmixturemlp_pa_t_e_kernel(
                     start=True,
                     stop=True,
                 )
-                nc.vector.tensor_copy(
+                nc.scalar.copy(
                     out=b2_all[:, m, BANK * half : BANK * (half + 1)].rearrange(
                         "b (u p e) -> b u p e", u=2, e=2
                     ),
@@ -253,36 +259,49 @@ def tile_gaussianmixturemlp_pa_t_e_kernel(
                 op=ALU.add,
             )
 
-        def closes_model(r):
-            return rounds[r][1] + rounds[r][2] == TILES
+        def part_closed_by(r):
+            m, first, count = rounds[r]
+            if first + count == WHOLE_ROUNDS:
+                return m, 0, WHOLE_ROUNDS
+            if first + count == TILES:
+                return m, WHOLE_ROUNDS, TILES
+            return None
 
         def head_functions(r):
-            if not closes_model(r):
+            if part_closed_by(r) is None:
                 return
-            y = held["y", rounds[r][0]]
+            m, lo, hi = part_closed_by(r)
+            means = held["y", m][:, lo:hi, 0:OUT]
+            raw = held["y", m][:, lo:hi, OUT:OUT2]
+            square = stage.tile([P, TILES, OUT], F32, tag="square")
+            positive = stage.tile([P, TILES, OUT], F32, tag="positive")
             size = stage.tile([P, TILES, OUT], F32, tag="size")
             decay = stage.tile([P, TILES, OUT], F32, tag="decay")
-            square = stage.tile([P, TILES, OUT], F32, tag="square")
-            nc.scalar.activation(out=size[:], in_=y[:, :, OUT:OUT2], func=ACT.Abs)
-            nc.scalar.activation(out=decay[:], in_=size[:], func=ACT.Exp, scale=-1.0)
-            nc.scalar.activation(out=square[:], in_=y[:, :, 0:OUT], func=ACT.Square)
-            held["decay", r] = decay
-            held["square", r] = square
+            nc.scalar.activation(out=square[:, lo:hi, :], in_=means, func=ACT.Square)
+            nc.scalar.activation(out=positive[:, lo:hi, :], in_=raw, func=ACT.Relu)
+            nc.scalar.activation(out=size[:, lo:hi, :], in_=raw, func=ACT.Abs)
+            nc.scalar.activation(out=decay[:, lo:hi, :], in_=size[:, lo:hi, :], func=ACT.Exp, scale=-1.0)
+            held["functions", r] = (square, positive, decay)
 
         def head_sums(r):
-            if not closes_model(r):
+            if part_closed_by(r) is None:
                 return
-            y = held["y", rounds[r][0]]
-            decay = held["decay", r]
-            square = held["square", r]
-            nc.gpsimd.tensor_tensor(out=mean_sum[:], in0=mean_sum[:], in1=y[:, :, 0:OUT], op=ALU.add)
+            m, lo, hi = part_closed_by(r)
+            square, positive, decay = held["functions", r]
             nc.vector.scalar_tensor_tensor(
-                out=var_sum[:], in0=y[:, :, OUT:OUT2], scalar=0.0, in1=var_sum[:], op0=ALU.max, op1=ALU.add
+                out=factors[:, lo:hi, :],
+                in0=decay[:, lo:hi, :],
+                scalar=1.0,
+                in1=factors[:, lo:hi, :],
+                op0=ALU.add,
+                op1=ALU.mult,
             )
-            nc.vector.scalar_tensor_tensor(
-                out=factors[:], in0=decay[:], scalar=1.0, in1=factors[:], op0=ALU.add, op1=ALU.mult
-            )
-            nc.vector.tensor_tensor(out=var_sum[:], in0=var_sum[:], in1=square[:], op=ALU.add)
+            for total, term in (
+                (mean_sum, held["y", m][:, lo:hi, 0:OUT]),
+                (var_sum, square[:, lo:hi, :]),
+                (var_sum, positive[:, lo:hi, :]),
+            ):
+                nc.gpsimd.tensor_tensor(out=total[:, lo:hi, :], in0=total[:, lo:hi, :], in1=term, op=ALU.add)
 
         def step(stage_of_round, r):
             if 0 <= r < len(rounds):
@@ -306,9 +325,11 @@ def tile_gaussianmixturemlp_pa_t_e_kernel(
         nc.vector.tensor_scalar_mul(out=mean[:], in0=mean_sum[:], scalar1=1.0 / MODELS)
         nc.sync.dma_start(out=out_0.rearrange("(p i) o -> p i o", i=TILES), in_=mean[:])
         nc.vector.tensor_tensor(out=mean_sq[:], in0=mean[:], in1=mean[:], op=ALU.mult)
-        nc.vector.tensor_tensor(out=var_sum[:], in0=var_sum[:], in1=log_sum[:], op=ALU.add)
         nc.vector.scalar_tensor_tensor(
             out=variance[:], in0=var_sum[:], scalar=1.0 / MODELS, in1=mean_sq[:], op0=ALU.mult, op1=ALU.subtract
+        )
+        nc.vector.scalar_tensor_tensor(
+            out=variance[:], in0=log_sum[:], scalar=1.0 / MODELS, in1=variance[:], op0=ALU.mult, op1=ALU.add
         )
         nc.vector.tensor_scalar(
             out=variance[:], in0=variance[:], scalar1=0.0, scalar2=EPS, op0=ALU.max, op1=ALU.add

@@ -29,8 +29,8 @@ HALVES = HIDDEN // BANK
 PLANES = 4
 
 ROUND = 2
-WHOLE_ROUNDS = TILES - TILES % ROUND
-H1_LEAD = 3
+Y_TILES = BANK // OUT2
+H1_LEAD = 2
 
 FLOPS = 2 * MODELS * BATCH * HIDDEN * (HIDDEN + OUT2)
 
@@ -68,9 +68,13 @@ def tile_gaussianmixturemlp_pa_t_e_kernel(
         b3_all = keep.tile([P, MODELS, OUT2], BF16)
         ident = keep.tile([P, P], F32)
         ident_bf = keep.tile([P, P], BF16)
+        one = keep.tile([P, 1], F32)
         mean_sum = keep.tile([P, TILES, OUT], F32)
         var_sum = keep.tile([P, TILES, OUT], F32)
         factors = keep.tile([P, TILES, OUT], F32)
+        mean = keep.tile([P, TILES, OUT], F32)
+        mean_sq = keep.tile([P, TILES, OUT], F32)
+        variance = keep.tile([P, TILES, OUT], F32)
 
         nc.vector.memset(w2_planes[:].bitcast(I32), 0)
         nc.vector.memset(w3_planes[:].bitcast(I32), 0)
@@ -78,6 +82,7 @@ def tile_gaussianmixturemlp_pa_t_e_kernel(
         nc.vector.memset(mean_sum[:], 0.0)
         nc.vector.memset(var_sum[:], MODELS * EPS)
         nc.vector.memset(factors[:], 1.0)
+        nc.vector.memset(one[:], 1.0)
         make_identity(nc, ident[:])
         nc.vector.tensor_copy(out=ident_bf[:], in_=ident[:])
 
@@ -87,11 +92,12 @@ def tile_gaussianmixturemlp_pa_t_e_kernel(
                 out=h1_sb[m][:, first : first + count, :], in_=rows[:, first : first + count, :]
             )
 
-        def load_w2(m):
+        def load_w2(m, half):
             c0 = PASSES * m
+            some = slice(PACK * BANK * half, PACK * BANK * (half + 1))
             nc.sync.dma_start(
-                out=w2_words[:, c0 : c0 + PASSES, :].bitcast(I32),
-                in_=W2_words[c0 : c0 + PASSES].rearrange("g p n t -> p g (n t)").bitcast(I32),
+                out=w2_words[:, c0 : c0 + PASSES, some].bitcast(I32),
+                in_=W2_words[c0 : c0 + PASSES].rearrange("g p n t -> p g (n t)")[:, :, some].bitcast(I32),
             )
 
         def load_w2_planes(c0):
@@ -104,15 +110,17 @@ def tile_gaussianmixturemlp_pa_t_e_kernel(
                     in_=W2_scales[c0 : c0 + n_planes, 4 * quadrant : 4 * quadrant + 4, :].bitcast(I32),
                 )
 
-        load_h1(0, 0, ROUND)
+        early = (H1_LEAD + 1) * ROUND
+        for first in range(0, early, ROUND):
+            load_h1(0, first, ROUND)
         nc.sync.dma_start(out=b2_rows[0:MODELS, :], in_=b2)
         load_w2_planes(0)
-        load_h1(0, ROUND, TILES - ROUND)
-        load_w2(0)
-        w3_planes_i32 = w3_planes[:].bitcast(I32)
+        for half in range(HALVES):
+            load_w2(0, half)
+        load_h1(0, early, TILES - early)
         for quadrant in range(4):
             nc.sync.dma_start(
-                out=w3_planes_i32[32 * quadrant : 32 * quadrant + 4, :, :],
+                out=w3_planes[:].bitcast(I32)[32 * quadrant : 32 * quadrant + 4, :, :],
                 in_=W3_scales[:, 4 * quadrant : 4 * quadrant + 4, :]
                 .rearrange("c r n -> r c n")
                 .bitcast(I32),
@@ -129,29 +137,32 @@ def tile_gaussianmixturemlp_pa_t_e_kernel(
             if (PASSES * m) % PLANES == 0:
                 load_w2_planes(PASSES * m)
             load_h1(m, 0, TILES)
-            load_w2(m)
+            for half in range(HALVES):
+                load_w2(m, half)
 
-        def sorted_view(columns):
+        held = {}
+
+        def in_sorted_order(columns):
             return columns.rearrange("b (p u e) -> b u p e", u=2, e=2)
 
-        for m in range(MODELS):
+        def as_sorted(columns):
+            return columns.rearrange("b (u p e) -> b u p e", u=2, e=2)
+
+        def spread_b2(r):
+            m, first, count = rounds[r]
+            if first != 0:
+                return
             for half in range(HALVES):
+                some = slice(BANK * half, BANK * (half + 1))
                 spread = psum_h2.tile([P, BANK], F32, tag="h2_bank")
                 nc.tensor.matmul(
                     out=spread[:],
                     lhsT=ident_bf[:, m : m + 1].to_broadcast([P, P]),
-                    rhs=b2_rows[:, BANK * half : BANK * (half + 1)],
+                    rhs=b2_rows[:, some],
                     start=True,
                     stop=True,
                 )
-                nc.scalar.copy(
-                    out=b2_all[:, m, BANK * half : BANK * (half + 1)].rearrange(
-                        "b (u p e) -> b u p e", u=2, e=2
-                    ),
-                    in_=sorted_view(spread[:]),
-                )
-
-        held = {}
+                nc.scalar.copy(out=as_sorted(b2_all[:, m, some]), in_=in_sorted_order(spread[:]))
 
         def transpose_h1(r):
             m, first, count = rounds[r]
@@ -190,6 +201,7 @@ def tile_gaussianmixturemlp_pa_t_e_kernel(
             h2 = stage.tile([P, ROUND, HALVES, BANK], BF16, tag="h2")
             for j in range(count):
                 for half in range(HALVES):
+                    some = slice(BANK * half, BANK * (half + 1))
                     bank = psum_h2.tile([P, BANK], F32, tag="h2_bank")
                     for g in range(PASSES):
                         c = PASSES * m + g
@@ -198,18 +210,14 @@ def tile_gaussianmixturemlp_pa_t_e_kernel(
                             lhsT=codes[:, j, g, :].bitcast(FP8X4),
                             lhsT_scale=scales[:, j, g, :],
                             rhs=w2_words[:, c, PACK * BANK * half : PACK * BANK * (half + 1)].bitcast(FP8X4),
-                            rhs_scale=w2_planes[
-                                4 * (c % PLANES) : P, c // PLANES, BANK * half : BANK * (half + 1)
-                            ],
+                            rhs_scale=w2_planes[4 * (c % PLANES) : P, c // PLANES, some],
                             start=(g == 0),
                             stop=(g == PASSES - 1),
                         )
                     nc.vector.tensor_tensor(
-                        out=h2[:, j, half, :].rearrange("b (u p e) -> b u p e", u=2, e=2),
-                        in0=sorted_view(bank[:]),
-                        in1=b2_all[:, m, BANK * half : BANK * (half + 1)].rearrange(
-                            "b (u p e) -> b u p e", u=2, e=2
-                        ),
+                        out=as_sorted(h2[:, j, half, :]),
+                        in0=in_sorted_order(bank[:]),
+                        in1=as_sorted(b2_all[:, m, some]),
                         op=ALU.add,
                     )
             held["h2", r] = h2
@@ -232,19 +240,27 @@ def tile_gaussianmixturemlp_pa_t_e_kernel(
                     )
             held["h2_grouped", r] = grouped
 
+        def y_part(r):
+            m, first, count = rounds[r]
+            lo = first - first % Y_TILES
+            return m, lo, min(lo + Y_TILES, TILES)
+
+        def closes_y_part(r):
+            return rounds[r][1] + rounds[r][2] == y_part(r)[2]
+
         def layer3(r):
             m, first, count = rounds[r]
+            lo, hi = y_part(r)[1:]
             codes, scales = held["h2_mx", r]
-            if first == 0:
-                y_new = stage.tile([P, TILES, OUT2], F32, tag="y")
-                held["y", m] = y_new
-            y = held["y", m]
-            y_bank = psum_y.tile([P, ROUND, OUT2], F32, tag="y_bank")
+            if first == lo:
+                y_new = psum_y.tile([P, Y_TILES, OUT2], F32, tag="y_bank")
+                held["y_bank", m, lo] = y_new
+            y_bank = held["y_bank", m, lo]
             for j in range(count):
                 for g in range(PASSES):
                     c = PASSES * m + g
                     nc.tensor.matmul_mx(
-                        out=y_bank[:, j, :],
+                        out=y_bank[:, first - lo + j, :],
                         lhsT=codes[:, j, g, :].bitcast(FP8X4),
                         lhsT_scale=scales[:, j, g, :],
                         rhs=w3_words[:, c, :].bitcast(FP8X4),
@@ -252,56 +268,72 @@ def tile_gaussianmixturemlp_pa_t_e_kernel(
                         start=(g == 0),
                         stop=(g == PASSES - 1),
                     )
-            nc.vector.tensor_tensor(
-                out=y[:, first : first + count, :],
-                in0=y_bank[:, 0:count, :],
-                in1=b3_all[:, m, :].unsqueeze(1).to_broadcast([P, count, OUT2]),
-                op=ALU.add,
-            )
-
-        def part_closed_by(r):
-            m, first, count = rounds[r]
-            if first + count == WHOLE_ROUNDS:
-                return m, 0, WHOLE_ROUNDS
-            if first + count == TILES:
-                return m, WHOLE_ROUNDS, TILES
-            return None
+            if closes_y_part(r):
+                y = stage.tile([P, Y_TILES, OUT2], F32, tag="y")
+                nc.vector.tensor_tensor(
+                    out=y[:, 0 : hi - lo, :],
+                    in0=y_bank[:, 0 : hi - lo, :],
+                    in1=b3_all[:, m, :].unsqueeze(1).to_broadcast([P, hi - lo, OUT2]),
+                    op=ALU.add,
+                )
+                held["y", r] = y
 
         def head_functions(r):
-            if part_closed_by(r) is None:
+            if not closes_y_part(r):
                 return
-            m, lo, hi = part_closed_by(r)
-            means = held["y", m][:, lo:hi, 0:OUT]
-            raw = held["y", m][:, lo:hi, OUT:OUT2]
-            square = stage.tile([P, TILES, OUT], F32, tag="square")
-            positive = stage.tile([P, TILES, OUT], F32, tag="positive")
-            size = stage.tile([P, TILES, OUT], F32, tag="size")
-            decay = stage.tile([P, TILES, OUT], F32, tag="decay")
-            nc.scalar.activation(out=square[:, lo:hi, :], in_=means, func=ACT.Square)
-            nc.scalar.activation(out=positive[:, lo:hi, :], in_=raw, func=ACT.Relu)
-            nc.scalar.activation(out=size[:, lo:hi, :], in_=raw, func=ACT.Abs)
-            nc.scalar.activation(out=decay[:, lo:hi, :], in_=size[:, lo:hi, :], func=ACT.Exp, scale=-1.0)
-            held["functions", r] = (square, positive, decay)
+            m, lo, hi = y_part(r)
+            n = hi - lo
+            y = held["y", r]
+            square = stage.tile([P, Y_TILES, OUT], F32, tag="square")
+            size = stage.tile([P, Y_TILES, OUT], F32, tag="size")
+            decay = stage.tile([P, Y_TILES, OUT], F32, tag="decay")
+            nc.scalar.activation(out=size[:, 0:n, :], in_=y[:, 0:n, OUT:OUT2], func=ACT.Abs)
+            nc.scalar.activation(out=decay[:, 0:n, :], in_=size[:, 0:n, :], func=ACT.Exp, scale=-1.0)
+            nc.scalar.activation(out=square[:, 0:n, :], in_=y[:, 0:n, 0:OUT], func=ACT.Square)
+            held["functions", r] = (square, decay)
 
         def head_sums(r):
-            if part_closed_by(r) is None:
+            if not closes_y_part(r):
                 return
-            m, lo, hi = part_closed_by(r)
-            square, positive, decay = held["functions", r]
+            m, lo, hi = y_part(r)
+            n = hi - lo
+            y = held["y", r]
+            square, decay = held["functions", r]
             nc.vector.scalar_tensor_tensor(
                 out=factors[:, lo:hi, :],
-                in0=decay[:, lo:hi, :],
+                in0=decay[:, 0:n, :],
                 scalar=1.0,
                 in1=factors[:, lo:hi, :],
                 op0=ALU.add,
                 op1=ALU.mult,
             )
-            for total, term in (
-                (mean_sum, held["y", m][:, lo:hi, 0:OUT]),
-                (var_sum, square[:, lo:hi, :]),
-                (var_sum, positive[:, lo:hi, :]),
-            ):
-                nc.gpsimd.tensor_tensor(out=total[:, lo:hi, :], in0=total[:, lo:hi, :], in1=term, op=ALU.add)
+            nc.vector.tensor_tensor(
+                out=mean_sum[:, lo:hi, :], in0=mean_sum[:, lo:hi, :], in1=y[:, 0:n, 0:OUT], op=ALU.add
+            )
+            nc.vector.scalar_tensor_tensor(
+                out=var_sum[:, lo:hi, :],
+                in0=y[:, 0:n, OUT:OUT2],
+                scalar=0.0,
+                in1=var_sum[:, lo:hi, :],
+                op0=ALU.max,
+                op1=ALU.add,
+            )
+            nc.vector.tensor_tensor(
+                out=var_sum[:, lo:hi, :], in0=var_sum[:, lo:hi, :], in1=square[:, 0:n, :], op=ALU.add
+            )
+            if m == MODELS - 1:
+                nc.vector.tensor_scalar_mul(out=mean[:, lo:hi, :], in0=mean_sum[:, lo:hi, :], scalar1=1.0 / MODELS)
+                nc.vector.tensor_tensor(
+                    out=mean_sq[:, lo:hi, :], in0=mean[:, lo:hi, :], in1=mean[:, lo:hi, :], op=ALU.mult
+                )
+                nc.vector.scalar_tensor_tensor(
+                    out=variance[:, lo:hi, :],
+                    in0=var_sum[:, lo:hi, :],
+                    scalar=1.0 / MODELS,
+                    in1=mean_sq[:, lo:hi, :],
+                    op0=ALU.mult,
+                    op1=ALU.subtract,
+                )
 
         def step(stage_of_round, r):
             if 0 <= r < len(rounds):
@@ -313,21 +345,16 @@ def tile_gaussianmixturemlp_pa_t_e_kernel(
             step(head_sums, s - H1_LEAD - 4)
             step(transpose_h1, s)
             step(transpose_h2, s - H1_LEAD - 1)
+            step(spread_b2, s - H1_LEAD + 1)
             step(layer2, s - H1_LEAD)
             step(layer3, s - H1_LEAD - 2)
             step(head_functions, s - H1_LEAD - 3)
 
+        log_one = keep.tile([P, 1], F32)
         log_sum = keep.tile([P, TILES, OUT], F32)
-        mean = keep.tile([P, TILES, OUT], F32)
-        mean_sq = keep.tile([P, TILES, OUT], F32)
-        variance = keep.tile([P, TILES, OUT], F32)
+        nc.scalar.activation(out=log_one[:], in_=one[:], func=ACT.Ln)
         nc.scalar.activation(out=log_sum[:], in_=factors[:], func=ACT.Ln)
-        nc.vector.tensor_scalar_mul(out=mean[:], in0=mean_sum[:], scalar1=1.0 / MODELS)
         nc.sync.dma_start(out=out_0.rearrange("(p i) o -> p i o", i=TILES), in_=mean[:])
-        nc.vector.tensor_tensor(out=mean_sq[:], in0=mean[:], in1=mean[:], op=ALU.mult)
-        nc.vector.scalar_tensor_tensor(
-            out=variance[:], in0=var_sum[:], scalar=1.0 / MODELS, in1=mean_sq[:], op0=ALU.mult, op1=ALU.subtract
-        )
         nc.vector.scalar_tensor_tensor(
             out=variance[:], in0=log_sum[:], scalar=1.0 / MODELS, in1=variance[:], op0=ALU.mult, op1=ALU.add
         )

@@ -1,3 +1,4 @@
+import math
 from contextlib import ExitStack
 
 import concourse.mybir as mybir
@@ -25,30 +26,37 @@ K_PASS = P * PACK
 PASSES = HIDDEN // K_PASS
 TILES = BATCH // P
 BANK = 512
-HALVES = HIDDEN // BANK
 PLANES = 4
 
-ROUND = 2
-Y_TILES = BANK // OUT2
-H1_LEAD = 2
+SLICES = ((0, 4), (4, 2), (6, 1))
+H1_BUFS = 3
+W2_BUFS = 3
 
 FLOPS = 2 * MODELS * BATCH * HIDDEN * (HIDDEN + OUT2)
 
 
-def rounds_of_row_tiles():
-    rounds = []
-    for m in range(MODELS):
-        for first in range(0, TILES, ROUND):
-            rounds.append((m, first, min(ROUND, TILES - first)))
-    return rounds
+def parts_of_the_batch():
+    parts = [(0, (2,)), (0, (1,)), (0, (0,))]
+    for m in range(1, MODELS - 1):
+        parts += [(m, (0,)), (m, (1, 2))]
+    parts += [(MODELS - 1, (0,)), (MODELS - 1, (1,)), (MODELS - 1, (2,))]
+    return parts
+
+
+def tiles_of(slices):
+    return SLICES[slices[0]][0], sum(SLICES[s][1] for s in slices)
 
 
 def tile_gaussianmixturemlp_pa_t_e_kernel(
     tc, h1, W2_words, W2_scales, b2, W3_words, W3_scales, b3, out_0, out_1
 ):
     nc = tc.nc
-    rounds = rounds_of_row_tiles()
     all_passes = MODELS * PASSES
+    plane_tiles = (all_passes + PLANES - 1) // PLANES
+    parts = parts_of_the_batch()
+    n_units = PASSES * len(parts)
+    first_unit = [min(PASSES * j for j in range(len(parts)) if parts[j][0] == m) for m in range(MODELS)]
+    last_part = [max(j for j in range(len(parts)) if parts[j][0] == m) for m in range(MODELS)]
 
     with ExitStack() as ctx:
         keep = ctx.enter_context(tc.tile_pool(name="keep", bufs=1))
@@ -58,16 +66,15 @@ def tile_gaussianmixturemlp_pa_t_e_kernel(
         psum_y = ctx.enter_context(tc.psum_pool(name="psum_y", bufs=1))
         ctx.enter_context(tc.manual_schedule())
 
-        h1_sb = [keep.tile([P, TILES, HIDDEN], BF16, name="h1_sb%d" % m) for m in range(MODELS)]
-        w2_words = keep.tile([P, all_passes, PACK * HIDDEN], U8, align_bytes=64)
+        w2_sorted = keep.tile([P, all_passes, PACK * HIDDEN], U8, align_bytes=64)
         w3_words = keep.tile([P, all_passes, PACK * OUT2], U8, align_bytes=64)
-        w2_planes = keep.tile([P, (all_passes + PLANES - 1) // PLANES, HIDDEN], U8, align_bytes=64)
+        w2_planes = keep.tile([P, plane_tiles, HIDDEN], U8, align_bytes=64)
+        w2_planes_sorted = keep.tile([P, plane_tiles, HIDDEN], U8, align_bytes=64)
         w3_planes = keep.tile([P, all_passes, OUT2], U8, align_bytes=64)
-        b2_rows = keep.tile([P, HIDDEN], BF16)
-        b2_all = keep.tile([P, MODELS, HIDDEN], BF16)
+        b2_bf = keep.tile([P, MODELS * PASSES, PACK], BF16)
+        b2_cols = keep.tile([P, MODELS * PASSES, PACK], F32)
         b3_all = keep.tile([P, MODELS, OUT2], BF16)
         ident = keep.tile([P, P], F32)
-        ident_bf = keep.tile([P, P], BF16)
         one = keep.tile([P, 1], F32)
         mean_sum = keep.tile([P, TILES, OUT], F32)
         var_sum = keep.tile([P, TILES, OUT], F32)
@@ -78,25 +85,28 @@ def tile_gaussianmixturemlp_pa_t_e_kernel(
 
         nc.vector.memset(w2_planes[:].bitcast(I32), 0)
         nc.vector.memset(w3_planes[:].bitcast(I32), 0)
-        nc.vector.memset(b2_rows[:], 0.0)
-        nc.vector.memset(mean_sum[:], 0.0)
-        nc.vector.memset(var_sum[:], MODELS * EPS)
-        nc.vector.memset(factors[:], 1.0)
         nc.vector.memset(one[:], 1.0)
         make_identity(nc, ident[:])
-        nc.vector.tensor_copy(out=ident_bf[:], in_=ident[:])
+
+        held = {}
 
         def load_h1(m, first, count):
+            if ("h1_rows", m) not in held:
+                h1_new = stage.tile([P, TILES, HIDDEN], BF16, tag="h1_rows", bufs=H1_BUFS)
+                held["h1_rows", m] = h1_new
             rows = h1[m].rearrange("(p i) k -> p i k", i=TILES)
             nc.sync.dma_start(
-                out=h1_sb[m][:, first : first + count, :], in_=rows[:, first : first + count, :]
+                out=held["h1_rows", m][:, first : first + count, :], in_=rows[:, first : first + count, :]
             )
 
-        def load_w2(m, half):
+        def load_w2(m, G):
+            if G == 0:
+                w2_new = stage.tile([P, PASSES, PACK * HIDDEN], U8, tag="w2_raw", bufs=W2_BUFS)
+                held["w2_raw", m] = w2_new
             c0 = PASSES * m
-            some = slice(PACK * BANK * half, PACK * BANK * (half + 1))
+            some = slice(PACK * BANK * G, PACK * BANK * (G + 1))
             nc.sync.dma_start(
-                out=w2_words[:, c0 : c0 + PASSES, some].bitcast(I32),
+                out=held["w2_raw", m][:, :, some].bitcast(I32),
                 in_=W2_words[c0 : c0 + PASSES].rearrange("g p n t -> p g (n t)")[:, :, some].bitcast(I32),
             )
 
@@ -110,195 +120,227 @@ def tile_gaussianmixturemlp_pa_t_e_kernel(
                     in_=W2_scales[c0 : c0 + n_planes, 4 * quadrant : 4 * quadrant + 4, :].bitcast(I32),
                 )
 
-        early = (H1_LEAD + 1) * ROUND
-        for first in range(0, early, ROUND):
-            load_h1(0, first, ROUND)
-        nc.sync.dma_start(out=b2_rows[0:MODELS, :], in_=b2)
-        load_w2_planes(0)
-        for half in range(HALVES):
-            load_w2(0, half)
-        load_h1(0, early, TILES - early)
-        for quadrant in range(4):
+        def load_w3():
+            for quadrant in range(4):
+                nc.sync.dma_start(
+                    out=w3_planes[:].bitcast(I32)[32 * quadrant : 32 * quadrant + 4, :, :],
+                    in_=W3_scales[:, 4 * quadrant : 4 * quadrant + 4, :]
+                    .rearrange("c r n -> r c n")
+                    .bitcast(I32),
+                )
             nc.sync.dma_start(
-                out=w3_planes[:].bitcast(I32)[32 * quadrant : 32 * quadrant + 4, :, :],
-                in_=W3_scales[:, 4 * quadrant : 4 * quadrant + 4, :]
-                .rearrange("c r n -> r c n")
-                .bitcast(I32),
+                out=w3_words[:].bitcast(I32),
+                in_=W3_words.rearrange("g p n t -> p g (n t)").bitcast(I32),
             )
-        nc.sync.dma_start(
-            out=w3_words[:].bitcast(I32),
-            in_=W3_words.rearrange("g p n t -> p g (n t)").bitcast(I32),
-        )
-        nc.sync.dma_start(
-            out=b3_all[:].rearrange("p m o -> p (m o)"),
-            in_=b3.rearrange("m o -> (m o)").partition_broadcast(P),
-        )
-        for m in range(1, MODELS):
-            if (PASSES * m) % PLANES == 0:
-                load_w2_planes(PASSES * m)
-            load_h1(m, 0, TILES)
-            for half in range(HALVES):
-                load_w2(m, half)
-
-        held = {}
-
-        def in_sorted_order(columns):
-            return columns.rearrange("b (p u e) -> b u p e", u=2, e=2)
-
-        def as_sorted(columns):
-            return columns.rearrange("b (u p e) -> b u p e", u=2, e=2)
-
-        def spread_b2(r):
-            m, first, count = rounds[r]
-            if first != 0:
-                return
-            for half in range(HALVES):
-                some = slice(BANK * half, BANK * (half + 1))
-                spread = psum_h2.tile([P, BANK], F32, tag="h2_bank")
-                nc.tensor.matmul(
-                    out=spread[:],
-                    lhsT=ident_bf[:, m : m + 1].to_broadcast([P, P]),
-                    rhs=b2_rows[:, some],
-                    start=True,
-                    stop=True,
-                )
-                nc.scalar.copy(out=as_sorted(b2_all[:, m, some]), in_=in_sorted_order(spread[:]))
-
-        def transpose_h1(r):
-            m, first, count = rounds[r]
-            words = h1_sb[m][:].bitcast(F32)
-            grouped = stage.tile([P, ROUND, PASSES, P, PACK], BF16, tag="h1_grouped", align_bytes=64)
-            for j in range(count):
-                flipped = psum_flip.tile([P, PASSES * 2, P], F32, tag="flipped")
-                for g in range(PASSES):
-                    for u in range(2):
-                        nc.tensor.transpose(
-                            flipped[:, 2 * g + u, :],
-                            words[:, first + j, 256 * g + u : 256 * (g + 1) : 2],
-                            ident[:],
-                        )
-                nc.scalar.copy(
-                    out=grouped[:, j].bitcast(F32),
-                    in_=flipped[:].rearrange("p (g u) b -> p g b u", u=2),
-                )
-            held["h1_grouped", r] = grouped
-
-        def quantise(r, what, bufs):
-            count = rounds[r][2]
-            grouped = held[what + "_grouped", r]
-            codes = stage.tile([P, ROUND, PASSES, P], U32, tag=what + "_codes", bufs=bufs, align_bytes=64)
-            scales = stage.tile([P, ROUND, PASSES, P], U8, tag=what + "_scales", bufs=bufs, align_bytes=64)
-            nc.vector.quantize_mx(
-                out=codes[:, 0:count].rearrange("p j g b -> p (j g b)").bitcast(FP8X4),
-                scales=scales[:, 0:count].rearrange("p j g b -> p (j g b)"),
-                in_=grouped[:, 0:count].rearrange("p j g b t -> p (j g b t)"),
+            nc.sync.dma_start(
+                out=b3_all[:].rearrange("p m o -> p (m o)"),
+                in_=b3.rearrange("m o -> (m o)").partition_broadcast(P),
             )
-            held[what + "_mx", r] = (codes, scales)
 
-        def layer2(r):
-            m, first, count = rounds[r]
-            codes, scales = held["h1_mx", r]
-            h2 = stage.tile([P, ROUND, HALVES, BANK], BF16, tag="h2")
-            for j in range(count):
-                for half in range(HALVES):
-                    some = slice(BANK * half, BANK * (half + 1))
-                    bank = psum_h2.tile([P, BANK], F32, tag="h2_bank")
+        nc.scalar.dma_start(
+            out=b2_bf[:], in_=b2.rearrange("m (g p t) -> p (m g) t", g=PASSES, t=PACK)
+        )
+        load_h1(0, 6, 1)
+        load_h1(0, 4, 2)
+        load_w2_planes(0)
+        load_w2(0, 0)
+        load_w2(0, 1)
+        load_h1(0, 0, 2)
+        load_h1(0, 2, 2)
+        load_w3()
+        load_h1(1, 0, 4)
+        load_w2(1, 0)
+        load_w2(1, 1)
+        load_h1(1, 4, 3)
+        load_w2_planes(PLANES)
+        load_h1(2, 0, TILES)
+        load_w2(2, 0)
+        load_w2(2, 1)
+        load_w2_planes(2 * PLANES)
+
+        def sort_w2(m, G):
+            c0 = PASSES * m
+            some = slice(PACK * BANK * G, PACK * BANK * (G + 1))
+            nc.vector.tensor_copy(
+                out=w2_sorted[:, c0 : c0 + PASSES, some].bitcast(I32).rearrange("p c (t i) -> p c t i", t=PACK),
+                in_=held["w2_raw", m][:, :, some].bitcast(I32).rearrange("p c (i t) -> p c t i", t=PACK),
+            )
+            if G == PASSES - 1 and m + W2_BUFS < MODELS:
+                for later_G in range(PASSES):
+                    load_w2(m + W2_BUFS, later_G)
+
+        def sort_w2_planes(tile_no):
+            nc.vector.tensor_copy(
+                out=w2_planes_sorted[:, tile_no, :].rearrange("p (g t i) -> p g t i", g=PASSES, t=PACK),
+                in_=w2_planes[:, tile_no, :].rearrange("p (g i t) -> p g t i", g=PASSES, t=PACK),
+            )
+
+        def transpose_h1(j):
+            m, slices = parts[j]
+            words = held["h1_rows", m][:].bitcast(F32)
+            for s in slices:
+                first, count = SLICES[s]
+                grouped = stage.tile(
+                    [P, PASSES, count, P, PACK], BF16, tag="h1_grouped%d" % s, bufs=1, align_bytes=64
+                )
+                for i in range(count):
+                    flipped = psum_flip.tile([P, PASSES * 2, P], F32, tag="flipped")
+                    for g in range(PASSES):
+                        for u in range(2):
+                            nc.tensor.transpose(
+                                flipped[:, 2 * g + u, :],
+                                words[:, first + i, 256 * g + u : 256 * (g + 1) : 2],
+                                ident[:],
+                            )
+                    nc.scalar.copy(
+                        out=grouped[:, :, i].bitcast(F32),
+                        in_=flipped[:].rearrange("p (g u) b -> p g b u", u=2),
+                    )
+                held["h1_grouped", m, s] = grouped
+            if j == last_part[m] and m + H1_BUFS < MODELS:
+                load_h1(m + H1_BUFS, 0, TILES)
+
+        def quantise_h1(j):
+            m, slices = parts[j]
+            for s in slices:
+                count = SLICES[s][1]
+                grouped = held["h1_grouped", m, s]
+                codes = stage.tile([P, PASSES, count * P], U32, tag="h1_codes%d" % s, align_bytes=64)
+                scales = stage.tile([P, PASSES, count * P], U8, tag="h1_scales%d" % s, align_bytes=64)
+                nc.vector.quantize_mx(
+                    out=codes[:].rearrange("p g c -> p (g c)").bitcast(FP8X4),
+                    scales=scales[:].rearrange("p g c -> p (g c)"),
+                    in_=grouped[:].rearrange("p g i b t -> p (g i b t)"),
+                )
+                held["h1_mx", m, s] = (codes, scales)
+
+        def layer2(k):
+            j, G = divmod(k, PASSES)
+            m, slices = parts[j]
+            width = P * tiles_of(slices)[1]
+            h2_rows = stage.tile([P, PACK, BANK], BF16, tag="h2_rows", bufs=3)
+            for t in range(PACK):
+                col = P * (PACK * G + t)
+                bank = psum_h2.tile([P, BANK], F32, tag="h2_bank")
+                at = 0
+                for s in slices:
+                    n = P * SLICES[s][1]
+                    codes, scales = held["h1_mx", m, s]
                     for g in range(PASSES):
                         c = PASSES * m + g
                         nc.tensor.matmul_mx(
-                            out=bank[:],
-                            lhsT=codes[:, j, g, :].bitcast(FP8X4),
-                            lhsT_scale=scales[:, j, g, :],
-                            rhs=w2_words[:, c, PACK * BANK * half : PACK * BANK * (half + 1)].bitcast(FP8X4),
-                            rhs_scale=w2_planes[4 * (c % PLANES) : P, c // PLANES, some],
+                            out=bank[:, at : at + n],
+                            lhsT=w2_sorted[:, c, PACK * col : PACK * (col + P)].bitcast(FP8X4),
+                            lhsT_scale=w2_planes_sorted[4 * (c % PLANES) : P, c // PLANES, col : col + P],
+                            rhs=codes[:, g, :].bitcast(FP8X4),
+                            rhs_scale=scales[:, g, :],
                             start=(g == 0),
                             stop=(g == PASSES - 1),
                         )
-                    nc.vector.tensor_tensor(
-                        out=as_sorted(h2[:, j, half, :]),
-                        in0=in_sorted_order(bank[:]),
-                        in1=as_sorted(b2_all[:, m, some]),
-                        op=ALU.add,
-                    )
-            held["h2", r] = h2
+                    at += n
+                nc.scalar.activation(
+                    out=h2_rows[:, t, 0:width],
+                    in_=bank[:, 0:width],
+                    func=ACT.Relu,
+                    bias=b2_cols[:, PASSES * m + G, t : t + 1],
+                )
+            held["h2_rows", k] = h2_rows
 
-        def transpose_h2(r):
-            count = rounds[r][2]
-            h2 = held["h2", r]
-            grouped = stage.tile([P, ROUND, PASSES, P, PACK], BF16, tag="h2_grouped", align_bytes=64)
-            for j in range(count):
-                words = h2[:, j].rearrange("b g n -> b (g n)").bitcast(F32)
-                flipped = psum_flip.tile([P, PASSES * 2, P], F32, tag="flipped")
-                for gu in range(PASSES * 2):
-                    nc.tensor.transpose(flipped[:, gu, :], words[:, P * gu : P * (gu + 1)], ident[:])
-                pairs = flipped[:].bitcast(BF16)
-                for g in range(PASSES):
-                    nc.scalar.activation(
-                        out=grouped[:, j, g].rearrange("p b (u e) -> p b u e", e=2),
-                        in_=pairs[:, 2 * g : 2 * g + 2, :].rearrange("p u (b e) -> p b u e", e=2),
-                        func=ACT.Relu,
-                    )
-            held["h2_grouped", r] = grouped
+        def interleave_h2(k):
+            j, G = divmod(k, PASSES)
+            width = P * tiles_of(parts[j][1])[1]
+            if G == 0:
+                new_grouped = stage.tile([P, PASSES, width, PACK], BF16, tag="h2_grouped", align_bytes=64)
+                held["h2_grouped", j] = new_grouped
+            nc.vector.tensor_copy(
+                out=held["h2_grouped", j][:, G],
+                in_=held["h2_rows", k][:, :, 0:width].rearrange("p t n -> p n t"),
+            )
 
-        def y_part(r):
-            m, first, count = rounds[r]
-            lo = first - first % Y_TILES
-            return m, lo, min(lo + Y_TILES, TILES)
+        def quantise_h2(j):
+            columns = PASSES * P * tiles_of(parts[j][1])[1]
+            codes = stage.tile([P, columns], U32, tag="h2_codes", align_bytes=64)
+            scales = stage.tile([P, columns], U8, tag="h2_scales", align_bytes=64)
+            flat = held["h2_grouped", j][:].rearrange("p g n t -> p (g n t)")
+            lo = 0
+            while lo < columns:
+                hi = lo + max(w for w in (128, 256, 512, 1024) if w <= columns - lo)
+                nc.vector.quantize_mx(
+                    out=codes[:, lo:hi].bitcast(FP8X4),
+                    scales=scales[:, lo:hi],
+                    in_=flat[:, PACK * lo : PACK * hi],
+                )
+                lo = hi
+            held["h2_mx", j] = (codes, scales)
 
-        def closes_y_part(r):
-            return rounds[r][1] + rounds[r][2] == y_part(r)[2]
-
-        def layer3(r):
-            m, first, count = rounds[r]
-            lo, hi = y_part(r)[1:]
-            codes, scales = held["h2_mx", r]
-            if first == lo:
-                y_new = psum_y.tile([P, Y_TILES, OUT2], F32, tag="y_bank")
-                held["y_bank", m, lo] = y_new
-            y_bank = held["y_bank", m, lo]
-            for j in range(count):
-                for g in range(PASSES):
-                    c = PASSES * m + g
+        def layer3(j):
+            m, slices = parts[j]
+            count = tiles_of(slices)[1]
+            codes, scales = held["h2_mx", j]
+            y_bank = psum_y.tile([P, BANK // OUT2, OUT2], F32, tag="y_bank")
+            for i in range(count):
+                for G in range(PASSES):
+                    c = PASSES * m + G
+                    cols = slice(P * (count * G + i), P * (count * G + i + 1))
                     nc.tensor.matmul_mx(
-                        out=y_bank[:, first - lo + j, :],
-                        lhsT=codes[:, j, g, :].bitcast(FP8X4),
-                        lhsT_scale=scales[:, j, g, :],
+                        out=y_bank[:, i, :],
+                        lhsT=codes[:, cols].bitcast(FP8X4),
+                        lhsT_scale=scales[:, cols],
                         rhs=w3_words[:, c, :].bitcast(FP8X4),
                         rhs_scale=w3_planes[:, c, :],
-                        start=(g == 0),
-                        stop=(g == PASSES - 1),
+                        start=(G == 0),
+                        stop=(G == PASSES - 1),
                     )
-            if closes_y_part(r):
-                y = stage.tile([P, Y_TILES, OUT2], F32, tag="y")
-                nc.vector.tensor_tensor(
-                    out=y[:, 0 : hi - lo, :],
-                    in0=y_bank[:, 0 : hi - lo, :],
-                    in1=b3_all[:, m, :].unsqueeze(1).to_broadcast([P, hi - lo, OUT2]),
-                    op=ALU.add,
-                )
-                held["y", r] = y
+            held["y_bank", j] = y_bank
 
-        def head_functions(r):
-            if not closes_y_part(r):
-                return
-            m, lo, hi = y_part(r)
-            n = hi - lo
-            y = held["y", r]
-            square = stage.tile([P, Y_TILES, OUT], F32, tag="square")
-            size = stage.tile([P, Y_TILES, OUT], F32, tag="size")
-            decay = stage.tile([P, Y_TILES, OUT], F32, tag="decay")
+        def add_b3(j):
+            m, slices = parts[j]
+            n = tiles_of(slices)[1]
+            y = stage.tile([P, BANK // OUT2, OUT2], F32, tag="y")
+            nc.vector.tensor_tensor(
+                out=y[:, 0:n, :],
+                in0=held["y_bank", j][:, 0:n, :],
+                in1=b3_all[:, m, :].unsqueeze(1).to_broadcast([P, n, OUT2]),
+                op=ALU.add,
+            )
+            held["y", j] = y
+
+        def head_functions(j):
+            n = tiles_of(parts[j][1])[1]
+            y = held["y", j]
+            square = stage.tile([P, BANK // OUT2, OUT], F32, tag="square")
+            size = stage.tile([P, BANK // OUT2, OUT], F32, tag="size")
+            decay = stage.tile([P, BANK // OUT2, OUT], F32, tag="decay")
             nc.scalar.activation(out=size[:, 0:n, :], in_=y[:, 0:n, OUT:OUT2], func=ACT.Abs)
             nc.scalar.activation(out=decay[:, 0:n, :], in_=size[:, 0:n, :], func=ACT.Exp, scale=-1.0)
             nc.scalar.activation(out=square[:, 0:n, :], in_=y[:, 0:n, 0:OUT], func=ACT.Square)
-            held["functions", r] = (square, decay)
+            held["functions", j] = (square, decay)
 
-        def head_sums(r):
-            if not closes_y_part(r):
+        def head_sums(j):
+            m, slices = parts[j]
+            lo, n = tiles_of(slices)
+            hi = lo + n
+            y = held["y", j]
+            square, decay = held["functions", j]
+            if m == 0:
+                nc.vector.tensor_scalar(
+                    out=factors[:, lo:hi, :],
+                    in0=decay[:, 0:n, :],
+                    scalar1=1.0,
+                    scalar2=math.exp(MODELS * EPS),
+                    op0=ALU.add,
+                    op1=ALU.mult,
+                )
+                nc.vector.tensor_copy(out=mean_sum[:, lo:hi, :], in_=y[:, 0:n, 0:OUT])
+                nc.vector.scalar_tensor_tensor(
+                    out=var_sum[:, lo:hi, :],
+                    in0=y[:, 0:n, OUT:OUT2],
+                    scalar=0.0,
+                    in1=square[:, 0:n, :],
+                    op0=ALU.max,
+                    op1=ALU.add,
+                )
                 return
-            m, lo, hi = y_part(r)
-            n = hi - lo
-            y = held["y", r]
-            square, decay = held["functions", r]
             nc.vector.scalar_tensor_tensor(
                 out=factors[:, lo:hi, :],
                 in0=decay[:, 0:n, :],
@@ -335,20 +377,42 @@ def tile_gaussianmixturemlp_pa_t_e_kernel(
                     op1=ALU.subtract,
                 )
 
-        def step(stage_of_round, r):
-            if 0 <= r < len(rounds):
-                stage_of_round(r)
+        def part(stage_of_part, j):
+            if 0 <= j < len(parts):
+                stage_of_part(j)
 
-        for s in range(len(rounds) + H1_LEAD + 4):
-            step(lambda r: quantise(r, "h1", H1_LEAD + 1), s - 1)
-            step(lambda r: quantise(r, "h2", 2), s - H1_LEAD - 2)
-            step(head_sums, s - H1_LEAD - 4)
-            step(transpose_h1, s)
-            step(transpose_h2, s - H1_LEAD - 1)
-            step(spread_b2, s - H1_LEAD + 1)
-            step(layer2, s - H1_LEAD)
-            step(layer3, s - H1_LEAD - 2)
-            step(head_functions, s - H1_LEAD - 3)
+        def unit(stage_of_unit, k):
+            if 0 <= k < n_units:
+                stage_of_unit(k)
+
+        nc.vector.tensor_copy(out=b2_cols[:], in_=b2_bf[:])
+        sort_w2_planes(0)
+        sort_w2(0, 0)
+        for k in range(-3, n_units + 9):
+            j, G = divmod(k, PASSES)
+            if G == 0:
+                part(head_sums, j - 4)
+            else:
+                part(add_b3, j - 2)
+                part(quantise_h2, j - 1)
+            unit(interleave_h2, k - 1)
+            for m in range(1, MODELS):
+                if k == first_unit[m] - 5 and (PASSES * m) % PLANES == 0:
+                    sort_w2_planes(PASSES * m // PLANES)
+                if k == first_unit[m] - 3:
+                    sort_w2(m, 0)
+                if k == first_unit[m] - 1:
+                    sort_w2(m, 1)
+            if G == 0:
+                part(quantise_h1, j + 1)
+                if k == 0:
+                    sort_w2(0, 1)
+                part(layer3, j - 2)
+            unit(layer2, k)
+            if G == 0:
+                part(head_functions, j - 3)
+            else:
+                part(transpose_h1, j + 2)
 
         log_one = keep.tile([P, 1], F32)
         log_sum = keep.tile([P, TILES, OUT], F32)

@@ -43,6 +43,17 @@ def parts_of_the_batch():
     return parts
 
 
+def head_groups(parts):
+    groups = []
+    for m in range(MODELS):
+        mine = [j for j in range(len(parts)) if parts[j][0] == m]
+        if m == MODELS - 1:
+            groups += [mine[:-1], mine[-1:]]
+        else:
+            groups.append(mine)
+    return groups
+
+
 def tiles_of(slices):
     return SLICES[slices[0]][0], sum(SLICES[s][1] for s in slices)
 
@@ -57,6 +68,8 @@ def tile_gaussianmixturemlp_pa_t_e_kernel(
     n_units = PASSES * len(parts)
     first_unit = [min(PASSES * j for j in range(len(parts)) if parts[j][0] == m) for m in range(MODELS)]
     last_part = [max(j for j in range(len(parts)) if parts[j][0] == m) for m in range(MODELS)]
+    groups = head_groups(parts)
+    group_of = dict((j, group) for group in groups for j in group)
 
     with ExitStack() as ctx:
         keep = ctx.enter_context(tc.tile_pool(name="keep", bufs=1))
@@ -147,8 +160,8 @@ def tile_gaussianmixturemlp_pa_t_e_kernel(
         load_w2(0, 1)
         load_h1(0, 0, 2)
         load_h1(0, 2, 2)
-        load_w3()
         load_h1(1, 0, 4)
+        load_w3()
         load_w2(1, 0)
         load_w2(1, 1)
         load_h1(1, 4, 3)
@@ -293,86 +306,84 @@ def tile_gaussianmixturemlp_pa_t_e_kernel(
                     )
             held["y_bank", j] = y_bank
 
+        def tiles_of_group(group):
+            firsts = [tiles_of(parts[j][1])[0] for j in group]
+            return min(firsts), max(tiles_of(parts[j][1])[0] + tiles_of(parts[j][1])[1] for j in group)
+
         def add_b3(j):
             m, slices = parts[j]
-            n = tiles_of(slices)[1]
-            y = stage.tile([P, BANK // OUT2, OUT2], F32, tag="y")
+            lo, n = tiles_of(slices)
+            last = group_of[j][-1]
+            if j == group_of[j][0]:
+                y_new = stage.tile([P, TILES, OUT2], F32, tag="y")
+                held["y", last] = y_new
             nc.vector.tensor_tensor(
-                out=y[:, 0:n, :],
+                out=held["y", last][:, lo : lo + n, :],
                 in0=held["y_bank", j][:, 0:n, :],
                 in1=b3_all[:, m, :].unsqueeze(1).to_broadcast([P, n, OUT2]),
                 op=ALU.add,
             )
-            held["y", j] = y
 
         def head_functions(j):
-            n = tiles_of(parts[j][1])[1]
+            if j != group_of[j][-1]:
+                return
+            lo, hi = tiles_of_group(group_of[j])
             y = held["y", j]
-            square = stage.tile([P, BANK // OUT2, OUT], F32, tag="square")
-            size = stage.tile([P, BANK // OUT2, OUT], F32, tag="size")
-            decay = stage.tile([P, BANK // OUT2, OUT], F32, tag="decay")
-            nc.scalar.activation(out=size[:, 0:n, :], in_=y[:, 0:n, OUT:OUT2], func=ACT.Abs)
-            nc.scalar.activation(out=decay[:, 0:n, :], in_=size[:, 0:n, :], func=ACT.Exp, scale=-1.0)
-            nc.scalar.activation(out=square[:, 0:n, :], in_=y[:, 0:n, 0:OUT], func=ACT.Square)
+            square = stage.tile([P, TILES, OUT], F32, tag="square")
+            size = stage.tile([P, TILES, OUT], F32, tag="size")
+            decay = stage.tile([P, TILES, OUT], F32, tag="decay")
+            nc.scalar.activation(out=size[:, lo:hi, :], in_=y[:, lo:hi, OUT:OUT2], func=ACT.Abs)
+            nc.scalar.activation(out=decay[:, lo:hi, :], in_=size[:, lo:hi, :], func=ACT.Exp, scale=-1.0)
+            nc.scalar.activation(out=square[:, lo:hi, :], in_=y[:, lo:hi, 0:OUT], func=ACT.Square)
             held["functions", j] = (square, decay)
 
         def head_sums(j):
-            m, slices = parts[j]
-            lo, n = tiles_of(slices)
-            hi = lo + n
+            if j != group_of[j][-1]:
+                return
+            m = parts[j][0]
+            lo, hi = tiles_of_group(group_of[j])
             y = held["y", j]
             square, decay = held["functions", j]
+            some = (slice(0, P), slice(lo, hi), slice(0, OUT))
+            means = y[:, lo:hi, 0:OUT]
+            raw = y[:, lo:hi, OUT:OUT2]
             if m == 0:
                 nc.vector.tensor_scalar(
-                    out=factors[:, lo:hi, :],
-                    in0=decay[:, 0:n, :],
+                    out=factors[some],
+                    in0=decay[some],
                     scalar1=1.0,
                     scalar2=math.exp(MODELS * EPS),
                     op0=ALU.add,
                     op1=ALU.mult,
                 )
-                nc.vector.tensor_copy(out=mean_sum[:, lo:hi, :], in_=y[:, 0:n, 0:OUT])
+                nc.vector.tensor_copy(out=mean_sum[some], in_=means)
                 nc.vector.scalar_tensor_tensor(
-                    out=var_sum[:, lo:hi, :],
-                    in0=y[:, 0:n, OUT:OUT2],
-                    scalar=0.0,
-                    in1=square[:, 0:n, :],
-                    op0=ALU.max,
-                    op1=ALU.add,
+                    out=var_sum[some], in0=raw, scalar=0.0, in1=square[some], op0=ALU.max, op1=ALU.add
                 )
                 return
             nc.vector.scalar_tensor_tensor(
-                out=factors[:, lo:hi, :],
-                in0=decay[:, 0:n, :],
-                scalar=1.0,
-                in1=factors[:, lo:hi, :],
-                op0=ALU.add,
-                op1=ALU.mult,
-            )
-            nc.vector.tensor_tensor(
-                out=mean_sum[:, lo:hi, :], in0=mean_sum[:, lo:hi, :], in1=y[:, 0:n, 0:OUT], op=ALU.add
+                out=var_sum[some], in0=raw, scalar=0.0, in1=var_sum[some], op0=ALU.max, op1=ALU.add
             )
             nc.vector.scalar_tensor_tensor(
-                out=var_sum[:, lo:hi, :],
-                in0=y[:, 0:n, OUT:OUT2],
-                scalar=0.0,
-                in1=var_sum[:, lo:hi, :],
-                op0=ALU.max,
-                op1=ALU.add,
+                out=factors[some], in0=decay[some], scalar=1.0, in1=factors[some], op0=ALU.add, op1=ALU.mult
             )
-            nc.vector.tensor_tensor(
-                out=var_sum[:, lo:hi, :], in0=var_sum[:, lo:hi, :], in1=square[:, 0:n, :], op=ALU.add
-            )
+            nc.vector.tensor_tensor(out=mean_sum[some], in0=mean_sum[some], in1=means, op=ALU.add)
+            nc.vector.tensor_tensor(out=var_sum[some], in0=var_sum[some], in1=square[some], op=ALU.add)
             if m == MODELS - 1:
-                nc.vector.tensor_scalar_mul(out=mean[:, lo:hi, :], in0=mean_sum[:, lo:hi, :], scalar1=1.0 / MODELS)
-                nc.vector.tensor_tensor(
-                    out=mean_sq[:, lo:hi, :], in0=mean[:, lo:hi, :], in1=mean[:, lo:hi, :], op=ALU.mult
-                )
                 nc.vector.scalar_tensor_tensor(
-                    out=variance[:, lo:hi, :],
-                    in0=var_sum[:, lo:hi, :],
+                    out=mean_sq[some],
+                    in0=mean_sum[some],
+                    scalar=1.0 / (MODELS * MODELS),
+                    in1=mean_sum[some],
+                    op0=ALU.mult,
+                    op1=ALU.mult,
+                )
+                nc.vector.tensor_scalar_mul(out=mean[some], in0=mean_sum[some], scalar1=1.0 / MODELS)
+                nc.vector.scalar_tensor_tensor(
+                    out=variance[some],
+                    in0=var_sum[some],
                     scalar=1.0 / MODELS,
-                    in1=mean_sq[:, lo:hi, :],
+                    in1=mean_sq[some],
                     op0=ALU.mult,
                     op1=ALU.subtract,
                 )

@@ -188,29 +188,31 @@ def tile_gaussianmixturemlp_pa_t_e_kernel(
                 in_=w2_planes[:, tile_no, :].rearrange("p (g i t) -> p g t i", g=PASSES, t=PACK),
             )
 
-        def transpose_h1(j):
+        def transpose_h1(j, half):
             m, slices = parts[j]
             words = held["h1_rows", m][:].bitcast(F32)
-            for s in slices:
+            mine = [(s, i) for s in slices for i in range(SLICES[s][1])]
+            cut = (len(mine) + 1) // 2
+            for s, i in mine[:cut] if half == 0 else mine[cut:]:
                 first, count = SLICES[s]
-                grouped = stage.tile(
-                    [P, PASSES, count, P, PACK], BF16, tag="h1_grouped%d" % s, bufs=1, align_bytes=64
-                )
-                for i in range(count):
-                    flipped = psum_flip.tile([P, PASSES * 2, P], F32, tag="flipped")
-                    for g in range(PASSES):
-                        for u in range(2):
-                            nc.tensor.transpose(
-                                flipped[:, 2 * g + u, :],
-                                words[:, first + i, 256 * g + u : 256 * (g + 1) : 2],
-                                ident[:],
-                            )
-                    nc.scalar.copy(
-                        out=grouped[:, :, i].bitcast(F32),
-                        in_=flipped[:].rearrange("p (g u) b -> p g b u", u=2),
+                if i == 0:
+                    grouped_new = stage.tile(
+                        [P, PASSES, count, P, PACK], BF16, tag="h1_grouped%d" % s, bufs=1, align_bytes=64
                     )
-                held["h1_grouped", m, s] = grouped
-            if j == last_part[m] and m + H1_BUFS < MODELS:
+                    held["h1_grouped", m, s] = grouped_new
+                flipped = psum_flip.tile([P, PASSES * 2, P], F32, tag="flipped")
+                for g in range(PASSES):
+                    for u in range(2):
+                        nc.tensor.transpose(
+                            flipped[:, 2 * g + u, :],
+                            words[:, first + i, 256 * g + u : 256 * (g + 1) : 2],
+                            ident[:],
+                        )
+                nc.scalar.copy(
+                    out=held["h1_grouped", m, s][:, :, i].bitcast(F32),
+                    in_=flipped[:].rearrange("p (g u) b -> p g b u", u=2),
+                )
+            if half == 1 and j == last_part[m] and m + H1_BUFS < MODELS:
                 load_h1(m + H1_BUFS, 0, TILES)
 
         def quantise_h1(j):
@@ -399,7 +401,7 @@ def tile_gaussianmixturemlp_pa_t_e_kernel(
         nc.vector.tensor_copy(out=b2_cols[:], in_=b2_bf[:])
         sort_w2_planes(0)
         sort_w2(0, 0)
-        for k in range(-3, n_units + 9):
+        for k in range(-4, n_units + 9):
             j, G = divmod(k, PASSES)
             if G == 0:
                 part(head_sums, j - 4)
@@ -420,10 +422,10 @@ def tile_gaussianmixturemlp_pa_t_e_kernel(
                     sort_w2(0, 1)
                 part(layer3, j - 2)
             unit(layer2, k)
+            if 0 <= j + 2 < len(parts):
+                transpose_h1(j + 2, G)
             if G == 0:
                 part(head_functions, j - 3)
-            else:
-                part(transpose_h1, j + 2)
 
         log_one = keep.tile([P, 1], F32)
         log_sum = keep.tile([P, TILES, OUT], F32)

@@ -268,8 +268,8 @@ def tile_gaussianmixturemlp_pa_t_e_kernel(
                 new_grouped = stage.tile([P, PASSES, width, PACK], BF16, tag="h2_grouped", align_bytes=64)
                 held["h2_grouped", j] = new_grouped
             nc.vector.tensor_copy(
-                out=held["h2_grouped", j][:, G],
-                in_=held["h2_rows", k][:, :, 0:width].rearrange("p t n -> p n t"),
+                out=held["h2_grouped", j][:, G].rearrange("p (c i) t -> p c t i", i=4),
+                in_=held["h2_rows", k][:, :, 0:width].rearrange("p t (c i) -> p c t i", i=4),
             )
 
         def quantise_h2(j):

@@ -133,7 +133,7 @@ def tile_gaussianmixturemlp_pa_t_e_kernel(
                     in_=W2_scales[c0 : c0 + n_planes, 4 * quadrant : 4 * quadrant + 4, :].bitcast(I32),
                 )
 
-        def load_w3():
+        def load_w3_planes():
             for quadrant in range(4):
                 nc.sync.dma_start(
                     out=w3_planes[:].bitcast(I32)[32 * quadrant : 32 * quadrant + 4, :, :],
@@ -141,10 +141,14 @@ def tile_gaussianmixturemlp_pa_t_e_kernel(
                     .rearrange("c r n -> r c n")
                     .bitcast(I32),
                 )
+
+        def load_w3(c0, c1):
             nc.sync.dma_start(
-                out=w3_words[:].bitcast(I32),
-                in_=W3_words.rearrange("g p n t -> p g (n t)").bitcast(I32),
+                out=w3_words[:, c0:c1, :].bitcast(I32),
+                in_=W3_words[c0:c1].rearrange("g p n t -> p g (n t)").bitcast(I32),
             )
+
+        def load_b3():
             nc.sync.dma_start(
                 out=b3_all[:].rearrange("p m o -> p (m o)"),
                 in_=b3.rearrange("m o -> (m o)").partition_broadcast(P),
@@ -153,23 +157,26 @@ def tile_gaussianmixturemlp_pa_t_e_kernel(
         nc.scalar.dma_start(
             out=b2_bf[:], in_=b2.rearrange("m (g p t) -> p (m g) t", g=PASSES, t=PACK)
         )
+        load_w2_planes(0)
         load_h1(0, 6, 1)
         load_h1(0, 4, 2)
-        load_w2_planes(0)
         load_w2(0, 0)
         load_w2(0, 1)
         load_h1(0, 0, 2)
         load_h1(0, 2, 2)
+        load_w3_planes()
+        load_w3(0, PASSES)
         load_h1(1, 0, 4)
-        load_w3()
+        load_b3()
         load_w2(1, 0)
         load_w2(1, 1)
         load_h1(1, 4, 3)
+        load_w3(PASSES, all_passes)
         load_w2_planes(PLANES)
+        load_w2_planes(2 * PLANES)
         load_h1(2, 0, TILES)
         load_w2(2, 0)
         load_w2(2, 1)
-        load_w2_planes(2 * PLANES)
 
         def sort_w2(m, G):
             c0 = PASSES * m

@@ -39,7 +39,7 @@ def parts_of_the_batch():
     parts = [(0, (2,)), (0, (1,)), (0, (0,))]
     for m in range(1, MODELS - 1):
         parts += [(m, (0,)), (m, (1, 2))]
-    parts += [(MODELS - 1, (0,)), (MODELS - 1, (1,)), (MODELS - 1, (2,))]
+    parts += [(MODELS - 1, (0,)), (MODELS - 1, (1, 2))]
     return parts
 
 
@@ -89,7 +89,6 @@ def tile_gaussianmixturemlp_pa_t_e_kernel(
         b3_all = keep.tile([P, MODELS, OUT2], BF16)
         ident = keep.tile([P, P], F32)
         one = keep.tile([P, 1], F32)
-        mean_sum = keep.tile([P, TILES, OUT], F32)
         var_sum = keep.tile([P, TILES, OUT], F32)
         factors = keep.tile([P, TILES, OUT], F32)
         mean = keep.tile([P, TILES, OUT], F32)
@@ -157,8 +156,8 @@ def tile_gaussianmixturemlp_pa_t_e_kernel(
         nc.scalar.dma_start(
             out=b2_bf[:], in_=b2.rearrange("m (g p t) -> p (m g) t", g=PASSES, t=PACK)
         )
-        load_w2_planes(0)
         load_h1(0, 6, 1)
+        load_w2_planes(0)
         load_h1(0, 4, 2)
         load_w2(0, 0)
         load_w2(0, 1)
@@ -365,29 +364,23 @@ def tile_gaussianmixturemlp_pa_t_e_kernel(
                     op0=ALU.add,
                     op1=ALU.mult,
                 )
-                nc.vector.tensor_copy(out=mean_sum[some], in_=means)
+                nc.vector.tensor_scalar_mul(out=mean[some], in0=means, scalar1=1.0 / MODELS)
                 nc.vector.scalar_tensor_tensor(
                     out=var_sum[some], in0=raw, scalar=0.0, in1=square[some], op0=ALU.max, op1=ALU.add
                 )
                 return
             nc.vector.scalar_tensor_tensor(
+                out=factors[some], in0=decay[some], scalar=1.0, in1=factors[some], op0=ALU.add, op1=ALU.mult
+            )
+            nc.vector.scalar_tensor_tensor(
                 out=var_sum[some], in0=raw, scalar=0.0, in1=var_sum[some], op0=ALU.max, op1=ALU.add
             )
             nc.vector.scalar_tensor_tensor(
-                out=factors[some], in0=decay[some], scalar=1.0, in1=factors[some], op0=ALU.add, op1=ALU.mult
+                out=mean[some], in0=means, scalar=1.0 / MODELS, in1=mean[some], op0=ALU.mult, op1=ALU.add
             )
-            nc.vector.tensor_tensor(out=mean_sum[some], in0=mean_sum[some], in1=means, op=ALU.add)
             nc.vector.tensor_tensor(out=var_sum[some], in0=var_sum[some], in1=square[some], op=ALU.add)
             if m == MODELS - 1:
-                nc.vector.scalar_tensor_tensor(
-                    out=mean_sq[some],
-                    in0=mean_sum[some],
-                    scalar=1.0 / (MODELS * MODELS),
-                    in1=mean_sum[some],
-                    op0=ALU.mult,
-                    op1=ALU.mult,
-                )
-                nc.vector.tensor_scalar_mul(out=mean[some], in0=mean_sum[some], scalar1=1.0 / MODELS)
+                nc.vector.tensor_tensor(out=mean_sq[some], in0=mean[some], in1=mean[some], op=ALU.mult)
                 nc.vector.scalar_tensor_tensor(
                     out=variance[some],
                     in0=var_sum[some],

@@ -32,6 +32,8 @@ SLICES = ((0, 4), (4, 2), (6, 1))
 H1_BUFS = 3
 W2_BUFS = 3
 
+FLIP_BANKS = 3
+
 FLOPS = 2 * MODELS * BATCH * HIDDEN * (HIDDEN + OUT2)
 
 
@@ -74,7 +76,7 @@ def tile_gaussianmixturemlp_pa_t_e_kernel(
     with ExitStack() as ctx:
         keep = ctx.enter_context(tc.tile_pool(name="keep", bufs=1))
         stage = ctx.enter_context(tc.tile_pool(name="stage", bufs=2))
-        psum_flip = ctx.enter_context(tc.psum_pool(name="psum_flip", bufs=3))
+        psum_flip = ctx.enter_context(tc.psum_pool(name="psum_flip", bufs=FLIP_BANKS))
         psum_h2 = ctx.enter_context(tc.psum_pool(name="psum_h2", bufs=4))
         psum_y = ctx.enter_context(tc.psum_pool(name="psum_y", bufs=1))
         ctx.enter_context(tc.manual_schedule())
@@ -198,7 +200,7 @@ def tile_gaussianmixturemlp_pa_t_e_kernel(
             m, slices = parts[j]
             words = held["h1_rows", m][:].bitcast(F32)
             mine = [(s, i) for s in slices for i in range(SLICES[s][1])]
-            cut = (len(mine) + 1) // 2
+            cut = len(mine) if len(mine) <= FLIP_BANKS else (len(mine) + 1) // 2
             for s, i in mine[:cut] if half == 0 else mine[cut:]:
                 first, count = SLICES[s]
                 if i == 0:

@@ -183,8 +183,8 @@ def tile_gaussianmixturemlp_pa_t_e_kernel(
             c0 = PASSES * m
             some = slice(PACK * BANK * G, PACK * BANK * (G + 1))
             nc.vector.tensor_copy(
-                out=w2_sorted[:, c0 : c0 + PASSES, some].bitcast(I32).rearrange("p c (t i) -> p c t i", t=PACK),
-                in_=held["w2_raw", m][:, :, some].bitcast(I32).rearrange("p c (i t) -> p c t i", t=PACK),
+                out=w2_sorted[:, c0 : c0 + PASSES, some].bitcast(I32).rearrange("p c (t i) -> p c i t", t=PACK),
+                in_=held["w2_raw", m][:, :, some].bitcast(I32).rearrange("p c (i t) -> p c i t", t=PACK),
             )
             if G == PASSES - 1 and m + W2_BUFS < MODELS:
                 for later_G in range(PASSES):

@@ -38,11 +38,7 @@ FLOPS = 2 * MODELS * BATCH * HIDDEN * (HIDDEN + OUT2)
 
 
 def parts_of_the_batch():
-    parts = [(0, (2,)), (0, (1,)), (0, (0,))]
-    for m in range(1, MODELS - 1):
-        parts += [(m, (0,)), (m, (1, 2))]
-    parts += [(MODELS - 1, (0,)), (MODELS - 1, (1, 2))]
-    return parts
+    return [(m, slices) for m in range(MODELS) for slices in ((0,), (1, 2))]
 
 
 def head_groups(parts):
@@ -155,23 +151,26 @@ def tile_gaussianmixturemlp_pa_t_e_kernel(
                 in_=b3.rearrange("m o -> (m o)").partition_broadcast(P),
             )
 
-        nc.scalar.dma_start(
-            out=b2_bf[:], in_=b2.rearrange("m (g p t) -> p (m g) t", g=PASSES, t=PACK)
-        )
-        load_h1(0, 6, 1)
+        def load_b2():
+            nc.sync.dma_start(
+                out=b2_bf[:], in_=b2.rearrange("m (g p t) -> p (m g) t", g=PASSES, t=PACK)
+            )
+
+        load_h1(0, 0, 1)
+        load_h1(0, 1, 1)
         load_w2_planes(0)
-        load_h1(0, 4, 2)
-        load_w2(0, 0)
-        load_w2(0, 1)
-        load_h1(0, 0, 2)
         load_h1(0, 2, 2)
+        load_w2(0, 0)
+        load_h1(0, 4, 3)
+        load_w2(0, 1)
+        load_b2()
         load_w3_planes()
         load_w3(0, PASSES)
         load_h1(1, 0, 4)
-        load_b3()
         load_w2(1, 0)
         load_w2(1, 1)
         load_h1(1, 4, 3)
+        load_b3()
         load_w3(PASSES, all_passes)
         load_w2_planes(PLANES)
         load_w2_planes(2 * PLANES)
@@ -216,7 +215,8 @@ def tile_gaussianmixturemlp_pa_t_e_kernel(
                             words[:, first + i, 256 * g + u : 256 * (g + 1) : 2],
                             ident[:],
                         )
-                nc.scalar.copy(
+                copy = nc.vector.tensor_copy if half == 1 and (s, i) == mine[cut] else nc.scalar.copy
+                copy(
                     out=held["h1_grouped", m, s][:, :, i].bitcast(F32),
                     in_=flipped[:].rearrange("p (g u) b -> p g b u", u=2),
                 )
@@ -400,9 +400,7 @@ def tile_gaussianmixturemlp_pa_t_e_kernel(
             if 0 <= k < n_units:
                 stage_of_unit(k)
 
-        nc.vector.tensor_copy(out=b2_cols[:], in_=b2_bf[:])
         sort_w2_planes(0)
-        sort_w2(0, 0)
         for k in range(-4, n_units + 9):
             j, G = divmod(k, PASSES)
             if G == 0:
@@ -418,10 +416,13 @@ def tile_gaussianmixturemlp_pa_t_e_kernel(
                     sort_w2(m, 0)
                 if k == first_unit[m] - 1:
                     sort_w2(m, 1)
+            if k == -1:
+                sort_w2(0, 0)
+                nc.vector.tensor_copy(out=b2_cols[:], in_=b2_bf[:])
+            if k == 0:
+                sort_w2(0, 1)
             if G == 0:
                 part(quantise_h1, j + 1)
-                if k == 0:
-                    sort_w2(0, 1)
                 part(layer3, j - 2)
             unit(layer2, k)
             if 0 <= j + 2 < len(parts):

@@ -86,7 +86,6 @@ def tile_gaussianmixturemlp_pa_t_e_kernel(
         b2_cols = keep.tile([P, MODELS * PASSES, PACK], F32)
         b3_all = keep.tile([P, MODELS, OUT2], BF16)
         ident = keep.tile([P, P], F32)
-        one = keep.tile([P, 1], F32)
         var_sum = keep.tile([P, TILES, OUT], F32)
         factors = keep.tile([P, TILES, OUT], F32)
         mean = keep.tile([P, TILES, OUT], F32)
@@ -95,7 +94,6 @@ def tile_gaussianmixturemlp_pa_t_e_kernel(
 
         nc.vector.memset(w2_planes[:].bitcast(I32), 0)
         nc.vector.memset(w3_planes[:].bitcast(I32), 0)
-        nc.vector.memset(one[:], 1.0)
         make_identity(nc, ident[:])
 
         held = {}
@@ -161,12 +159,14 @@ def tile_gaussianmixturemlp_pa_t_e_kernel(
         load_w2_planes(0)
         load_h1(0, 2, 2)
         load_w2(0, 0)
-        load_h1(0, 4, 3)
+        load_h1(0, 4, 2)
+        load_h1(0, 6, 1)
         load_w2(0, 1)
         load_b2()
+        load_h1(1, 0, 2)
+        load_h1(1, 2, 2)
         load_w3_planes()
         load_w3(0, PASSES)
-        load_h1(1, 0, 4)
         load_w2(1, 0)
         load_w2(1, 1)
         load_h1(1, 4, 3)
@@ -325,7 +325,7 @@ def tile_gaussianmixturemlp_pa_t_e_kernel(
             lo, n = tiles_of(slices)
             last = group_of[j][-1]
             if j == group_of[j][0]:
-                y_new = stage.tile([P, TILES, OUT2], F32, tag="y")
+                y_new = stage.tile([P, TILES, OUT2], F32, tag="y", bufs=3)
                 held["y", last] = y_new
             nc.vector.tensor_tensor(
                 out=held["y", last][:, lo : lo + n, :],
@@ -339,25 +339,23 @@ def tile_gaussianmixturemlp_pa_t_e_kernel(
                 return
             lo, hi = tiles_of_group(group_of[j])
             y = held["y", j]
-            square = stage.tile([P, TILES, OUT], F32, tag="square")
+            square = stage.tile([P, TILES, OUT], F32, tag="square", bufs=3)
             size = stage.tile([P, TILES, OUT], F32, tag="size")
-            decay = stage.tile([P, TILES, OUT], F32, tag="decay")
+            decay = stage.tile([P, TILES, OUT], F32, tag="decay", bufs=3)
             nc.scalar.activation(out=size[:, lo:hi, :], in_=y[:, lo:hi, OUT:OUT2], func=ACT.Abs)
-            nc.scalar.activation(out=decay[:, lo:hi, :], in_=size[:, lo:hi, :], func=ACT.Exp, scale=-1.0)
             nc.scalar.activation(out=square[:, lo:hi, :], in_=y[:, lo:hi, 0:OUT], func=ACT.Square)
+            nc.scalar.activation(out=decay[:, lo:hi, :], in_=size[:, lo:hi, :], func=ACT.Exp, scale=-1.0)
             held["functions", j] = (square, decay)
 
-        def head_sums(j):
-            if j != group_of[j][-1]:
-                return
-            m = parts[j][0]
+        def piece(j):
             lo, hi = tiles_of_group(group_of[j])
-            y = held["y", j]
-            square, decay = held["functions", j]
             some = (slice(0, P), slice(lo, hi), slice(0, OUT))
-            means = y[:, lo:hi, 0:OUT]
-            raw = y[:, lo:hi, OUT:OUT2]
-            if m == 0:
+            return some, held["y", j][:, lo:hi, 0:OUT], held["y", j][:, lo:hi, OUT:OUT2]
+
+        def take_product(j):
+            some = piece(j)[0]
+            decay = held["functions", j][1]
+            if parts[j][0] == 0:
                 nc.vector.tensor_scalar(
                     out=factors[some],
                     in0=decay[some],
@@ -366,31 +364,38 @@ def tile_gaussianmixturemlp_pa_t_e_kernel(
                     op0=ALU.add,
                     op1=ALU.mult,
                 )
-                nc.vector.tensor_scalar_mul(out=mean[some], in0=means, scalar1=1.0 / MODELS)
-                nc.vector.scalar_tensor_tensor(
-                    out=var_sum[some], in0=raw, scalar=0.0, in1=square[some], op0=ALU.max, op1=ALU.add
-                )
                 return
             nc.vector.scalar_tensor_tensor(
                 out=factors[some], in0=decay[some], scalar=1.0, in1=factors[some], op0=ALU.add, op1=ALU.mult
             )
+
+        def take_relu(j):
+            some, means, raw = piece(j)
+            other = held["functions", j][0] if parts[j][0] == 0 else var_sum
             nc.vector.scalar_tensor_tensor(
-                out=var_sum[some], in0=raw, scalar=0.0, in1=var_sum[some], op0=ALU.max, op1=ALU.add
+                out=var_sum[some], in0=raw, scalar=0.0, in1=other[some], op0=ALU.max, op1=ALU.add
             )
+
+        def take_mean(j):
+            some, means, raw = piece(j)
+            if parts[j][0] == 0:
+                nc.vector.tensor_scalar_mul(out=mean[some], in0=means, scalar1=1.0 / MODELS)
+                return
             nc.vector.scalar_tensor_tensor(
                 out=mean[some], in0=means, scalar=1.0 / MODELS, in1=mean[some], op0=ALU.mult, op1=ALU.add
             )
-            nc.vector.tensor_tensor(out=var_sum[some], in0=var_sum[some], in1=square[some], op=ALU.add)
-            if m == MODELS - 1:
-                nc.vector.tensor_tensor(out=mean_sq[some], in0=mean[some], in1=mean[some], op=ALU.mult)
-                nc.vector.scalar_tensor_tensor(
-                    out=variance[some],
-                    in0=var_sum[some],
-                    scalar=1.0 / MODELS,
-                    in1=mean_sq[some],
-                    op0=ALU.mult,
-                    op1=ALU.subtract,
+
+        def take_square(j):
+            some = piece(j)[0]
+            if parts[j][0] > 0:
+                nc.vector.tensor_tensor(
+                    out=var_sum[some], in0=var_sum[some], in1=held["functions", j][0][some], op=ALU.add
                 )
+
+        def head_sums(j):
+            if j == group_of[j][-1]:
+                for take in (take_product, take_relu, take_mean, take_square):
+                    take(j)
 
         def part(stage_of_part, j):
             if 0 <= j < len(parts):
@@ -401,7 +406,8 @@ def tile_gaussianmixturemlp_pa_t_e_kernel(
                 stage_of_unit(k)
 
         sort_w2_planes(0)
-        for k in range(-4, n_units + 9):
+        last = len(parts) - 1
+        for k in range(-4, n_units + PASSES):
             j, G = divmod(k, PASSES)
             if G == 0:
                 part(head_sums, j - 4)
@@ -430,15 +436,39 @@ def tile_gaussianmixturemlp_pa_t_e_kernel(
             if G == 0:
                 part(head_functions, j - 3)
 
-        log_one = keep.tile([P, 1], F32)
         log_sum = keep.tile([P, TILES, OUT], F32)
-        nc.scalar.activation(out=log_one[:], in_=one[:], func=ACT.Ln)
-        nc.scalar.activation(out=log_sum[:], in_=factors[:], func=ACT.Ln)
+        before, ahead = last - 1, last - 2
+        layer3(last)
+        head_functions(before)
+        take_product(ahead)
+        take_relu(ahead)
+        add_b3(last)
+        head_functions(last)
+        take_mean(ahead)
+        take_square(ahead)
+        for j in (before, last):
+            take_product(j)
+            take_relu(j)
+            take_mean(j)
+            take_square(j)
+            some = piece(j)[0]
+            nc.scalar.activation(out=log_sum[some], in_=factors[some], func=ACT.Ln)
         nc.sync.dma_start(out=out_0.rearrange("(p i) o -> p i o", i=TILES), in_=mean[:])
+        nc.vector.tensor_tensor(out=mean_sq[:], in0=mean[:], in1=mean[:], op=ALU.mult)
         nc.vector.scalar_tensor_tensor(
-            out=variance[:], in0=log_sum[:], scalar=1.0 / MODELS, in1=variance[:], op0=ALU.mult, op1=ALU.add
+            out=variance[:], in0=var_sum[:], scalar=1.0 / MODELS, in1=mean_sq[:], op0=ALU.mult, op1=ALU.subtract,
         )
-        nc.vector.tensor_scalar(
-            out=variance[:], in0=variance[:], scalar1=0.0, scalar2=EPS, op0=ALU.max, op1=ALU.add
-        )
-        nc.sync.dma_start(out=out_1.rearrange("(p i) o -> p i o", i=TILES), in_=variance[:])
+        for j in (before, last):
+            some = piece(j)[0]
+            nc.vector.scalar_tensor_tensor(
+                out=variance[some], in0=log_sum[some], scalar=1.0 / MODELS, in1=variance[some], op0=ALU.mult, op1=ALU.add
+            )
+        for j in (before, last):
+            some = piece(j)[0]
+            lo, hi = tiles_of_group(group_of[j])
+            nc.vector.tensor_scalar(
+                out=variance[some], in0=variance[some], scalar1=0.0, scalar2=EPS, op0=ALU.max, op1=ALU.add
+            )
+            nc.sync.dma_start(
+                out=out_1.rearrange("(p i) o -> p i o", i=TILES)[:, lo:hi, :], in_=variance[:, lo:hi, :]
+            )

@@ -32,6 +32,7 @@ SLICES = ((0, 4), (4, 2), (6, 1))
 H1_BUFS = 3
 W2_BUFS = 3
 
+FOLD_FROM = 3
 FLIP_BANKS = 3
 
 FLOPS = 2 * MODELS * BATCH * HIDDEN * (HIDDEN + OUT2)
@@ -39,17 +40,6 @@ FLOPS = 2 * MODELS * BATCH * HIDDEN * (HIDDEN + OUT2)
 
 def parts_of_the_batch():
     return [(m, slices) for m in range(MODELS) for slices in ((0,), (1, 2))]
-
-
-def head_groups(parts):
-    groups = []
-    for m in range(MODELS):
-        mine = [j for j in range(len(parts)) if parts[j][0] == m]
-        if m == MODELS - 1:
-            groups += [mine[:-1], mine[-1:]]
-        else:
-            groups.append(mine)
-    return groups
 
 
 def tiles_of(slices):
@@ -66,8 +56,7 @@ def tile_gaussianmixturemlp_pa_t_e_kernel(
     n_units = PASSES * len(parts)
     first_unit = [min(PASSES * j for j in range(len(parts)) if parts[j][0] == m) for m in range(MODELS)]
     last_part = [max(j for j in range(len(parts)) if parts[j][0] == m) for m in range(MODELS)]
-    groups = head_groups(parts)
-    group_of = dict((j, group) for group in groups for j in group)
+    last = len(parts) - 1
 
     with ExitStack() as ctx:
         keep = ctx.enter_context(tc.tile_pool(name="keep", bufs=1))
@@ -86,7 +75,9 @@ def tile_gaussianmixturemlp_pa_t_e_kernel(
         b2_cols = keep.tile([P, MODELS * PASSES, PACK], F32)
         b3_all = keep.tile([P, MODELS, OUT2], BF16)
         ident = keep.tile([P, P], F32)
+        fifth = keep.tile([P, P], F32)
         var_sum = keep.tile([P, TILES, OUT], F32)
+        mean_sum = keep.tile([P, TILES, OUT], F32)
         factors = keep.tile([P, TILES, OUT], F32)
         mean = keep.tile([P, TILES, OUT], F32)
         mean_sq = keep.tile([P, TILES, OUT], F32)
@@ -95,6 +86,7 @@ def tile_gaussianmixturemlp_pa_t_e_kernel(
         nc.vector.memset(w2_planes[:].bitcast(I32), 0)
         nc.vector.memset(w3_planes[:].bitcast(I32), 0)
         make_identity(nc, ident[:])
+        nc.vector.tensor_scalar_mul(out=fifth[:], in0=ident[:], scalar1=1.0 / MODELS)
 
         held = {}
 
@@ -316,86 +308,83 @@ def tile_gaussianmixturemlp_pa_t_e_kernel(
                     )
             held["y_bank", j] = y_bank
 
-        def tiles_of_group(group):
-            firsts = [tiles_of(parts[j][1])[0] for j in group]
-            return min(firsts), max(tiles_of(parts[j][1])[0] + tiles_of(parts[j][1])[1] for j in group)
-
         def add_b3(j):
             m, slices = parts[j]
-            lo, n = tiles_of(slices)
-            last = group_of[j][-1]
-            if j == group_of[j][0]:
-                y_new = stage.tile([P, TILES, OUT2], F32, tag="y", bufs=3)
-                held["y", last] = y_new
+            n = tiles_of(slices)[1]
+            y = stage.tile([P, BANK // OUT2, OUT2], F32, tag="y", bufs=7)
+            held["y", j] = y
             nc.vector.tensor_tensor(
-                out=held["y", last][:, lo : lo + n, :],
+                out=y[:, 0:n, :],
                 in0=held["y_bank", j][:, 0:n, :],
                 in1=b3_all[:, m, :].unsqueeze(1).to_broadcast([P, n, OUT2]),
                 op=ALU.add,
             )
 
         def head_functions(j):
-            if j != group_of[j][-1]:
-                return
-            lo, hi = tiles_of_group(group_of[j])
+            n = tiles_of(parts[j][1])[1]
             y = held["y", j]
-            square = stage.tile([P, TILES, OUT], F32, tag="square", bufs=3)
-            size = stage.tile([P, TILES, OUT], F32, tag="size")
-            decay = stage.tile([P, TILES, OUT], F32, tag="decay", bufs=3)
-            nc.scalar.activation(out=size[:, lo:hi, :], in_=y[:, lo:hi, OUT:OUT2], func=ACT.Abs)
-            nc.scalar.activation(out=square[:, lo:hi, :], in_=y[:, lo:hi, 0:OUT], func=ACT.Square)
-            nc.scalar.activation(out=decay[:, lo:hi, :], in_=size[:, lo:hi, :], func=ACT.Exp, scale=-1.0)
+            size = stage.tile([P, BANK // OUT2, OUT], F32, tag="size", bufs=2)
+            square = stage.tile([P, BANK // OUT2, OUT], F32, tag="square", bufs=5)
+            decay = stage.tile([P, BANK // OUT2, OUT], F32, tag="decay", bufs=5)
+            nc.scalar.activation(out=size[:, 0:n, :], in_=y[:, 0:n, OUT:OUT2], func=ACT.Abs)
+            nc.scalar.activation(out=square[:, 0:n, :], in_=y[:, 0:n, 0:OUT], func=ACT.Square)
+            nc.scalar.activation(out=decay[:, 0:n, :], in_=size[:, 0:n, :], func=ACT.Exp, scale=-1.0)
             held["functions", j] = (square, decay)
 
-        def piece(j):
-            lo, hi = tiles_of_group(group_of[j])
-            some = (slice(0, P), slice(lo, hi), slice(0, OUT))
-            return some, held["y", j][:, lo:hi, 0:OUT], held["y", j][:, lo:hi, OUT:OUT2]
+        def part_of(tile, j):
+            lo, n = tiles_of(parts[j][1])
+            return tile[:, lo : lo + n, :]
 
-        def take_product(j):
-            some = piece(j)[0]
-            decay = held["functions", j][1]
-            if parts[j][0] == 0:
+        def head_sums(j):
+            m, slices = parts[j]
+            n = tiles_of(slices)[1]
+            means = held["y", j][:, 0:n, 0:OUT]
+            raw = held["y", j][:, 0:n, OUT:OUT2]
+            square, decay = [tile[:, 0:n, :] for tile in held["functions", j]]
+            if m == 0:
                 nc.vector.tensor_scalar(
-                    out=factors[some],
-                    in0=decay[some],
+                    out=part_of(factors, j),
+                    in0=decay,
                     scalar1=1.0,
                     scalar2=math.exp(MODELS * EPS),
                     op0=ALU.add,
                     op1=ALU.mult,
                 )
-                return
-            nc.vector.scalar_tensor_tensor(
-                out=factors[some], in0=decay[some], scalar=1.0, in1=factors[some], op0=ALU.add, op1=ALU.mult
-            )
-
-        def take_relu(j):
-            some, means, raw = piece(j)
-            other = held["functions", j][0] if parts[j][0] == 0 else var_sum
-            nc.vector.scalar_tensor_tensor(
-                out=var_sum[some], in0=raw, scalar=0.0, in1=other[some], op0=ALU.max, op1=ALU.add
-            )
-
-        def take_mean(j):
-            some, means, raw = piece(j)
-            if parts[j][0] == 0:
-                nc.vector.tensor_scalar_mul(out=mean[some], in0=means, scalar1=1.0 / MODELS)
-                return
-            nc.vector.scalar_tensor_tensor(
-                out=mean[some], in0=means, scalar=1.0 / MODELS, in1=mean[some], op0=ALU.mult, op1=ALU.add
-            )
-
-        def take_square(j):
-            some = piece(j)[0]
-            if parts[j][0] > 0:
-                nc.vector.tensor_tensor(
-                    out=var_sum[some], in0=var_sum[some], in1=held["functions", j][0][some], op=ALU.add
+                nc.vector.tensor_copy(out=part_of(mean_sum, j), in_=means)
+                nc.vector.scalar_tensor_tensor(
+                    out=part_of(var_sum, j), in0=raw, scalar=0.0, in1=square, op0=ALU.max, op1=ALU.add
                 )
+                return
+            nc.vector.scalar_tensor_tensor(
+                out=part_of(factors, j), in0=decay, scalar=1.0, in1=part_of(factors, j), op0=ALU.add, op1=ALU.mult
+            )
+            if m >= FOLD_FROM:
+                spread = stage.tile([P, BANK // OUT2, OUT], F32, tag="spread", bufs=6)
+                held["spread", j] = spread
+                nc.vector.scalar_tensor_tensor(
+                    out=spread[:, 0:n, :], in0=raw, scalar=0.0, in1=square, op0=ALU.max, op1=ALU.add
+                )
+                return
+            nc.vector.scalar_tensor_tensor(
+                out=part_of(var_sum, j), in0=raw, scalar=0.0, in1=part_of(var_sum, j), op0=ALU.max, op1=ALU.add
+            )
+            nc.vector.tensor_tensor(out=part_of(mean_sum, j), in0=part_of(mean_sum, j), in1=means, op=ALU.add)
+            nc.vector.tensor_tensor(out=part_of(var_sum, j), in0=part_of(var_sum, j), in1=square, op=ALU.add)
 
-        def head_sums(j):
-            if j == group_of[j][-1]:
-                for take in (take_product, take_relu, take_mean, take_square):
-                    take(j)
+        def fold(what, j):
+            m, slices = parts[j]
+            n = tiles_of(slices)[1]
+            if m == FOLD_FROM:
+                pool, tag = (psum_h2, "h2_bank") if (what, slices[0]) == ("spread", 1) else (psum_flip, "flipped")
+                sums_new = pool.tile([P, BANK // OUT, OUT], F32, tag=tag)
+                held[what, "sums", slices] = sums_new
+                first_models = mean_sum if what == "y" else var_sum
+            sums = held[what, "sums", slices][:, 0:n, :]
+            if m == FOLD_FROM:
+                nc.tensor.matmul(sums, lhsT=fifth[:], rhs=part_of(first_models, j), start=True, stop=False)
+            nc.tensor.matmul(
+                sums, lhsT=fifth[:], rhs=held[what, j][:, 0:n, 0:OUT], start=False, stop=(m == MODELS - 1)
+            )
 
         def part(stage_of_part, j):
             if 0 <= j < len(parts):
@@ -406,15 +395,14 @@ def tile_gaussianmixturemlp_pa_t_e_kernel(
                 stage_of_unit(k)
 
         sort_w2_planes(0)
-        last = len(parts) - 1
         for k in range(-4, n_units + PASSES):
             j, G = divmod(k, PASSES)
-            if G == 0:
-                part(head_sums, j - 4)
-            else:
+            if G == 1:
                 part(add_b3, j - 2)
                 part(quantise_h2, j - 1)
             unit(interleave_h2, k - 1)
+            if G == 1:
+                part(head_sums, j - 4)
             for m in range(1, MODELS):
                 if k == first_unit[m] - 5 and (PASSES * m) % PLANES == 0:
                     sort_w2_planes(PASSES * m // PLANES)
@@ -433,42 +421,52 @@ def tile_gaussianmixturemlp_pa_t_e_kernel(
             unit(layer2, k)
             if 0 <= j + 2 < len(parts):
                 transpose_h1(j + 2, G)
-            if G == 0:
+            if G == 1:
                 part(head_functions, j - 3)
+            if k == n_units:
+                fold("y", 6)
+                fold("y", 7)
 
         log_sum = keep.tile([P, TILES, OUT], F32)
         before, ahead = last - 1, last - 2
+        fold("y", before)
         layer3(last)
         head_functions(before)
-        take_product(ahead)
-        take_relu(ahead)
+        mean_tile = held["y", "sums", parts[before][1]]
+        n = tiles_of(parts[before][1])[1]
+        nc.scalar.copy(out=part_of(mean, before), in_=mean_tile[:, 0:n, :])
+        nc.scalar.activation(out=part_of(mean_sq, before), in_=mean_tile[:, 0:n, :], func=ACT.Square)
+        head_sums(ahead)
+        fold("spread", ahead - 1)
+        fold("spread", ahead)
         add_b3(last)
         head_functions(last)
-        take_mean(ahead)
-        take_square(ahead)
+        fold("y", last)
         for j in (before, last):
-            take_product(j)
-            take_relu(j)
-            take_mean(j)
-            take_square(j)
-            some = piece(j)[0]
-            nc.scalar.activation(out=log_sum[some], in_=factors[some], func=ACT.Ln)
+            head_sums(j)
+            fold("spread", j)
+            nc.scalar.activation(out=part_of(log_sum, j), in_=part_of(factors, j), func=ACT.Ln)
+        n = tiles_of(parts[last][1])[1]
+        nc.vector.tensor_copy(out=part_of(mean, last), in_=held["y", "sums", parts[last][1]][:, 0:n, :])
         nc.sync.dma_start(out=out_0.rearrange("(p i) o -> p i o", i=TILES), in_=mean[:])
-        nc.vector.tensor_tensor(out=mean_sq[:], in0=mean[:], in1=mean[:], op=ALU.mult)
-        nc.vector.scalar_tensor_tensor(
-            out=variance[:], in0=var_sum[:], scalar=1.0 / MODELS, in1=mean_sq[:], op0=ALU.mult, op1=ALU.subtract,
-        )
+        nc.vector.tensor_tensor(out=part_of(mean_sq, last), in0=part_of(mean, last), in1=part_of(mean, last), op=ALU.mult)
         for j in (before, last):
-            some = piece(j)[0]
-            nc.vector.scalar_tensor_tensor(
-                out=variance[some], in0=log_sum[some], scalar=1.0 / MODELS, in1=variance[some], op0=ALU.mult, op1=ALU.add
+            n = tiles_of(parts[j][1])[1]
+            nc.vector.tensor_tensor(
+                out=part_of(variance, j),
+                in0=held["spread", "sums", parts[j][1]][:, 0:n, :],
+                in1=part_of(mean_sq, j),
+                op=ALU.subtract,
             )
         for j in (before, last):
-            some = piece(j)[0]
-            lo, hi = tiles_of_group(group_of[j])
+            nc.vector.scalar_tensor_tensor(
+                out=part_of(variance, j), in0=part_of(log_sum, j), scalar=1.0 / MODELS, in1=part_of(variance, j), op0=ALU.mult, op1=ALU.add
+            )
+        for j in (before, last):
+            lo, n = tiles_of(parts[j][1])
             nc.vector.tensor_scalar(
-                out=variance[some], in0=variance[some], scalar1=0.0, scalar2=EPS, op0=ALU.max, op1=ALU.add
+                out=part_of(variance, j), in0=part_of(variance, j), scalar1=0.0, scalar2=EPS, op0=ALU.max, op1=ALU.add
             )
             nc.sync.dma_start(
-                out=out_1.rearrange("(p i) o -> p i o", i=TILES)[:, lo:hi, :], in_=variance[:, lo:hi, :]
+                out=out_1.rearrange("(p i) o -> p i o", i=TILES)[:, lo : lo + n, :], in_=part_of(variance, j)
             )

@@ -163,10 +163,11 @@ def tile_gaussianmixturemlp_pa_t_e_kernel(
         load_w2(1, 1)
         load_h1(1, 4, 3)
         load_b3()
+        load_h1(2, 0, 4)
         load_w3(PASSES, all_passes)
         load_w2_planes(PLANES)
         load_w2_planes(2 * PLANES)
-        load_h1(2, 0, TILES)
+        load_h1(2, 4, 3)
         load_w2(2, 0)
         load_w2(2, 1)
 
@@ -187,33 +188,54 @@ def tile_gaussianmixturemlp_pa_t_e_kernel(
                 in_=w2_planes[:, tile_no, :].rearrange("p (g i t) -> p g t i", g=PASSES, t=PACK),
             )
 
-        def transpose_h1(j, half):
-            m, slices = parts[j]
-            words = held["h1_rows", m][:].bitcast(F32)
-            mine = [(s, i) for s in slices for i in range(SLICES[s][1])]
+        def rows_behind(k):
+            j, half = divmod(k, PASSES)
+            if not 0 <= j + 2 < len(parts):
+                return []
+            m, slices = parts[j + 2]
+            mine = [(m, s, i) for s in slices for i in range(SLICES[s][1])]
             cut = len(mine) if len(mine) <= FLIP_BANKS else (len(mine) + 1) // 2
-            for s, i in mine[:cut] if half == 0 else mine[cut:]:
-                first, count = SLICES[s]
+            return mine[:cut] if half == 0 else mine[cut:]
+
+        def words_of(m, s, i):
+            return held["h1_rows", m][:].bitcast(F32)[:, SLICES[s][0] + i, :]
+
+        def split_words(k):
+            if k % PASSES == 0:
+                for m, s, i in rows_behind(k)[:2]:
+                    if m in (1, 2):
+                        split_new = stage.tile([P, PASSES, 2, P], F32, tag="h1_split", bufs=4)
+                        nc.vector.tensor_copy(
+                            out=split_new[:], in_=words_of(m, s, i).rearrange("p (g w u) -> p g u w", g=PASSES, u=2)
+                        )
+                        held["h1_split", m, s, i] = split_new
+
+        def transpose_h1(k):
+            rows = rows_behind(k)
+            for m, s, i in rows:
                 if i == 0:
                     grouped_new = stage.tile(
-                        [P, PASSES, count, P, PACK], BF16, tag="h1_grouped%d" % s, bufs=1, align_bytes=64
+                        [P, PASSES, SLICES[s][1], P, PACK], BF16, tag="h1_grouped%d" % s, bufs=1, align_bytes=64
                     )
                     held["h1_grouped", m, s] = grouped_new
                 flipped = psum_flip.tile([P, PASSES * 2, P], F32, tag="flipped")
                 for g in range(PASSES):
                     for u in range(2):
-                        nc.tensor.transpose(
-                            flipped[:, 2 * g + u, :],
-                            words[:, first + i, 256 * g + u : 256 * (g + 1) : 2],
-                            ident[:],
-                        )
-                copy = nc.vector.tensor_copy if half == 1 and (s, i) == mine[cut] else nc.scalar.copy
+                        if ("h1_split", m, s, i) in held:
+                            words = held["h1_split", m, s, i][:, g, u, :]
+                        else:
+                            words = words_of(m, s, i)[:, 256 * g + u : 256 * (g + 1) : 2]
+                        nc.tensor.transpose(flipped[:, 2 * g + u, :], words, ident[:])
+                copy = nc.vector.tensor_copy if k % PASSES == 1 and (m, s, i) == rows[0] else nc.scalar.copy
                 copy(
                     out=held["h1_grouped", m, s][:, :, i].bitcast(F32),
                     in_=flipped[:].rearrange("p (g u) b -> p g b u", u=2),
                 )
-            if half == 1 and j == last_part[m] and m + H1_BUFS < MODELS:
-                load_h1(m + H1_BUFS, 0, TILES)
+            j, half = divmod(k, PASSES)
+            if half == 1 and 0 <= j + 2 < len(parts) and j + 2 == last_part[parts[j + 2][0]]:
+                m = parts[j + 2][0]
+                if m + H1_BUFS < MODELS:
+                    load_h1(m + H1_BUFS, 0, TILES)
 
         def quantise_h1(j):
             m, slices = parts[j]
@@ -311,7 +333,7 @@ def tile_gaussianmixturemlp_pa_t_e_kernel(
         def add_b3(j):
             m, slices = parts[j]
             n = tiles_of(slices)[1]
-            y = stage.tile([P, BANK // OUT2, OUT2], F32, tag="y", bufs=7)
+            y = stage.tile([P, BANK // OUT2, OUT2], F32, tag="y", bufs=5)
             held["y", j] = y
             nc.vector.tensor_tensor(
                 out=y[:, 0:n, :],
@@ -324,8 +346,8 @@ def tile_gaussianmixturemlp_pa_t_e_kernel(
             n = tiles_of(parts[j][1])[1]
             y = held["y", j]
             size = stage.tile([P, BANK // OUT2, OUT], F32, tag="size", bufs=2)
-            square = stage.tile([P, BANK // OUT2, OUT], F32, tag="square", bufs=5)
-            decay = stage.tile([P, BANK // OUT2, OUT], F32, tag="decay", bufs=5)
+            square = stage.tile([P, BANK // OUT2, OUT], F32, tag="square", bufs=3)
+            decay = stage.tile([P, BANK // OUT2, OUT], F32, tag="decay", bufs=3)
             nc.scalar.activation(out=size[:, 0:n, :], in_=y[:, 0:n, OUT:OUT2], func=ACT.Abs)
             nc.scalar.activation(out=square[:, 0:n, :], in_=y[:, 0:n, 0:OUT], func=ACT.Square)
             nc.scalar.activation(out=decay[:, 0:n, :], in_=size[:, 0:n, :], func=ACT.Exp, scale=-1.0)
@@ -359,7 +381,7 @@ def tile_gaussianmixturemlp_pa_t_e_kernel(
                 out=part_of(factors, j), in0=decay, scalar=1.0, in1=part_of(factors, j), op0=ALU.add, op1=ALU.mult
             )
             if m >= FOLD_FROM:
-                spread = stage.tile([P, BANK // OUT2, OUT], F32, tag="spread", bufs=6)
+                spread = stage.tile([P, BANK // OUT2, OUT], F32, tag="spread", bufs=4)
                 held["spread", j] = spread
                 nc.vector.scalar_tensor_tensor(
                     out=spread[:, 0:n, :], in0=raw, scalar=0.0, in1=square, op0=ALU.max, op1=ALU.add
@@ -418,9 +440,9 @@ def tile_gaussianmixturemlp_pa_t_e_kernel(
             if G == 0:
                 part(quantise_h1, j + 1)
                 part(layer3, j - 2)
+            split_words(k + 1)
             unit(layer2, k)
-            if 0 <= j + 2 < len(parts):
-                transpose_h1(j + 2, G)
+            transpose_h1(k)
             if G == 1:
                 part(head_functions, j - 3)
             if k == n_units:

@@ -32,8 +32,9 @@ SLICES = ((0, 4), (4, 2), (6, 1))
 H1_BUFS = 3
 W2_BUFS = 3
 
-FOLD_FROM = 3
+FOLD_FROM = MODELS - 2
 FLIP_BANKS = 3
+AHEAD = 2
 
 FLOPS = 2 * MODELS * BATCH * HIDDEN * (HIDDEN + OUT2)
 
@@ -100,13 +101,12 @@ def tile_gaussianmixturemlp_pa_t_e_kernel(
             )
 
         def load_w2(m, G):
-            if G == 0:
-                w2_new = stage.tile([P, PASSES, PACK * HIDDEN], U8, tag="w2_raw", bufs=W2_BUFS)
-                held["w2_raw", m] = w2_new
+            w2_new = stage.tile([P, PASSES, PACK * BANK], U8, tag="w2_raw%d" % G, bufs=W2_BUFS)
+            held["w2_raw", m, G] = w2_new
             c0 = PASSES * m
             some = slice(PACK * BANK * G, PACK * BANK * (G + 1))
             nc.sync.dma_start(
-                out=held["w2_raw", m][:, :, some].bitcast(I32),
+                out=w2_new[:].bitcast(I32),
                 in_=W2_words[c0 : c0 + PASSES].rearrange("g p n t -> p g (n t)")[:, :, some].bitcast(I32),
             )
 
@@ -150,18 +150,18 @@ def tile_gaussianmixturemlp_pa_t_e_kernel(
         load_h1(0, 1, 1)
         load_w2_planes(0)
         load_h1(0, 2, 2)
-        load_w2(0, 0)
         load_h1(0, 4, 2)
+        load_w2(0, 0)
         load_h1(0, 6, 1)
-        load_w2(0, 1)
         load_b2()
+        load_w2(0, 1)
         load_h1(1, 0, 2)
         load_h1(1, 2, 2)
+        load_w2(1, 0)
+        load_h1(1, 4, 3)
+        load_w2(1, 1)
         load_w3_planes()
         load_w3(0, PASSES)
-        load_w2(1, 0)
-        load_w2(1, 1)
-        load_h1(1, 4, 3)
         load_b3()
         load_h1(2, 0, 4)
         load_w3(PASSES, all_passes)
@@ -176,11 +176,10 @@ def tile_gaussianmixturemlp_pa_t_e_kernel(
             some = slice(PACK * BANK * G, PACK * BANK * (G + 1))
             nc.vector.tensor_copy(
                 out=w2_sorted[:, c0 : c0 + PASSES, some].bitcast(I32).rearrange("p c (t i) -> p c i t", t=PACK),
-                in_=held["w2_raw", m][:, :, some].bitcast(I32).rearrange("p c (i t) -> p c i t", t=PACK),
+                in_=held["w2_raw", m, G][:].bitcast(I32).rearrange("p c (i t) -> p c i t", t=PACK),
             )
-            if G == PASSES - 1 and m + W2_BUFS < MODELS:
-                for later_G in range(PASSES):
-                    load_w2(m + W2_BUFS, later_G)
+            if m + W2_BUFS < MODELS:
+                load_w2(m + W2_BUFS, G)
 
         def sort_w2_planes(tile_no):
             nc.vector.tensor_copy(
@@ -190,9 +189,9 @@ def tile_gaussianmixturemlp_pa_t_e_kernel(
 
         def rows_behind(k):
             j, half = divmod(k, PASSES)
-            if not 0 <= j + 2 < len(parts):
+            if not 0 <= j + AHEAD < len(parts):
                 return []
-            m, slices = parts[j + 2]
+            m, slices = parts[j + AHEAD]
             mine = [(m, s, i) for s in slices for i in range(SLICES[s][1])]
             cut = len(mine) if len(mine) <= FLIP_BANKS else (len(mine) + 1) // 2
             return mine[:cut] if half == 0 else mine[cut:]
@@ -203,10 +202,11 @@ def tile_gaussianmixturemlp_pa_t_e_kernel(
         def split_words(k):
             if k % PASSES == 0:
                 for m, s, i in rows_behind(k)[:2]:
-                    if m in (1, 2):
+                    if m == 2 or (m == 1 and s > 0):
                         split_new = stage.tile([P, PASSES, 2, P], F32, tag="h1_split", bufs=4)
                         nc.vector.tensor_copy(
-                            out=split_new[:], in_=words_of(m, s, i).rearrange("p (g w u) -> p g u w", g=PASSES, u=2)
+                            out=split_new[:],
+                            in_=words_of(m, s, i).rearrange("p (g w u) -> p g u w", g=PASSES, u=2),
                         )
                         held["h1_split", m, s, i] = split_new
 
@@ -224,32 +224,41 @@ def tile_gaussianmixturemlp_pa_t_e_kernel(
                         if ("h1_split", m, s, i) in held:
                             words = held["h1_split", m, s, i][:, g, u, :]
                         else:
-                            words = words_of(m, s, i)[:, 256 * g + u : 256 * (g + 1) : 2]
+                            words = words_of(m, s, i)[:, 2 * P * g + u : 2 * P * (g + 1) : 2]
                         nc.tensor.transpose(flipped[:, 2 * g + u, :], words, ident[:])
                 copy = nc.vector.tensor_copy if k % PASSES == 1 and (m, s, i) == rows[0] else nc.scalar.copy
                 copy(
                     out=held["h1_grouped", m, s][:, :, i].bitcast(F32),
                     in_=flipped[:].rearrange("p (g u) b -> p g b u", u=2),
                 )
-            j, half = divmod(k, PASSES)
-            if half == 1 and 0 <= j + 2 < len(parts) and j + 2 == last_part[parts[j + 2][0]]:
-                m = parts[j + 2][0]
-                if m + H1_BUFS < MODELS:
-                    load_h1(m + H1_BUFS, 0, TILES)
+            j = k // PASSES + AHEAD
+            if k % PASSES == 1 and j in last_part and parts[j][0] + H1_BUFS < MODELS:
+                load_h1(parts[j][0] + H1_BUFS, 0, TILES)
 
-        def quantise_h1(j):
+        def quantise_h1(j, half=None):
             m, slices = parts[j]
             for s in slices:
                 count = SLICES[s][1]
                 grouped = held["h1_grouped", m, s]
-                codes = stage.tile([P, PASSES, count * P], U32, tag="h1_codes%d" % s, align_bytes=64)
-                scales = stage.tile([P, PASSES, count * P], U8, tag="h1_scales%d" % s, align_bytes=64)
-                nc.vector.quantize_mx(
-                    out=codes[:].rearrange("p g c -> p (g c)").bitcast(FP8X4),
-                    scales=scales[:].rearrange("p g c -> p (g c)"),
-                    in_=grouped[:].rearrange("p g i b t -> p (g i b t)"),
-                )
-                held["h1_mx", m, s] = (codes, scales)
+                if half != 1:
+                    codes_new = stage.tile([P, PASSES, count * P], U32, tag="h1_codes%d" % s, align_bytes=64)
+                    scales_new = stage.tile([P, PASSES, count * P], U8, tag="h1_scales%d" % s, align_bytes=64)
+                    held["h1_mx", m, s] = (codes_new, scales_new)
+                codes, scales = held["h1_mx", m, s]
+                if half is None:
+                    nc.vector.quantize_mx(
+                        out=codes[:].rearrange("p g c -> p (g c)").bitcast(FP8X4),
+                        scales=scales[:].rearrange("p g c -> p (g c)"),
+                        in_=grouped[:].rearrange("p g i b t -> p (g i b t)"),
+                    )
+                    continue
+                lo, hi = half * count // 2, (half + 1) * count // 2
+                for g in range(PASSES):
+                    nc.vector.quantize_mx(
+                        out=codes[:, g, P * lo : P * hi].bitcast(FP8X4),
+                        scales=scales[:, g, P * lo : P * hi],
+                        in_=grouped[:, g, lo:hi].rearrange("p i b t -> p (i b t)"),
+                    )
 
         def layer2(k):
             j, G = divmod(k, PASSES)
@@ -393,19 +402,29 @@ def tile_gaussianmixturemlp_pa_t_e_kernel(
             nc.vector.tensor_tensor(out=part_of(mean_sum, j), in0=part_of(mean_sum, j), in1=means, op=ALU.add)
             nc.vector.tensor_tensor(out=part_of(var_sum, j), in0=part_of(var_sum, j), in1=square, op=ALU.add)
 
+        def sums_of(what, j):
+            return held[what, "sums", parts[j][1]][:, 0 : tiles_of(parts[j][1])[1], :]
+
         def fold(what, j):
             m, slices = parts[j]
             n = tiles_of(slices)[1]
             if m == FOLD_FROM:
-                pool, tag = (psum_h2, "h2_bank") if (what, slices[0]) == ("spread", 1) else (psum_flip, "flipped")
+                if what == "spread" and slices[0] > 0:
+                    pool, tag = psum_h2, "h2_bank"
+                else:
+                    pool, tag = psum_flip, "flipped"
                 sums_new = pool.tile([P, BANK // OUT, OUT], F32, tag=tag)
                 held[what, "sums", slices] = sums_new
                 first_models = mean_sum if what == "y" else var_sum
-            sums = held[what, "sums", slices][:, 0:n, :]
-            if m == FOLD_FROM:
-                nc.tensor.matmul(sums, lhsT=fifth[:], rhs=part_of(first_models, j), start=True, stop=False)
+                nc.tensor.matmul(
+                    sums_of(what, j), lhsT=fifth[:], rhs=part_of(first_models, j), start=True, stop=False
+                )
             nc.tensor.matmul(
-                sums, lhsT=fifth[:], rhs=held[what, j][:, 0:n, 0:OUT], start=False, stop=(m == MODELS - 1)
+                sums_of(what, j),
+                lhsT=fifth[:],
+                rhs=held[what, j][:, 0:n, 0:OUT],
+                start=False,
+                stop=(m == MODELS - 1),
             )
 
         def part(stage_of_part, j):
@@ -416,8 +435,10 @@ def tile_gaussianmixturemlp_pa_t_e_kernel(
             if 0 <= k < n_units:
                 stage_of_unit(k)
 
+        before = last - 1
+        ahead = [j for j in range(before) if parts[j][0] == MODELS - 2]
         sort_w2_planes(0)
-        for k in range(-4, n_units + PASSES):
+        for k in range(-PASSES * AHEAD, n_units + PASSES):
             j, G = divmod(k, PASSES)
             if G == 1:
                 part(add_b3, j - 2)
@@ -432,13 +453,17 @@ def tile_gaussianmixturemlp_pa_t_e_kernel(
                     sort_w2(m, 0)
                 if k == first_unit[m] - 1:
                     sort_w2(m, 1)
-            if k == -1:
+            if k == -3:
+                quantise_h1(0, 0)
+            if k == -2:
                 sort_w2(0, 0)
+                quantise_h1(0, 1)
+            if k == -1:
                 nc.vector.tensor_copy(out=b2_cols[:], in_=b2_bf[:])
-            if k == 0:
                 sort_w2(0, 1)
             if G == 0:
-                part(quantise_h1, j + 1)
+                if j >= 0:
+                    part(quantise_h1, j + 1)
                 part(layer3, j - 2)
             split_words(k + 1)
             unit(layer2, k)
@@ -446,49 +471,53 @@ def tile_gaussianmixturemlp_pa_t_e_kernel(
             if G == 1:
                 part(head_functions, j - 3)
             if k == n_units:
-                fold("y", 6)
-                fold("y", 7)
+                for j in ahead:
+                    fold("y", j)
 
         log_sum = keep.tile([P, TILES, OUT], F32)
-        before, ahead = last - 1, last - 2
+        ends = (before, last)
         fold("y", before)
         layer3(last)
         head_functions(before)
-        mean_tile = held["y", "sums", parts[before][1]]
-        n = tiles_of(parts[before][1])[1]
-        nc.scalar.copy(out=part_of(mean, before), in_=mean_tile[:, 0:n, :])
-        nc.scalar.activation(out=part_of(mean_sq, before), in_=mean_tile[:, 0:n, :], func=ACT.Square)
-        head_sums(ahead)
-        fold("spread", ahead - 1)
-        fold("spread", ahead)
+        nc.scalar.copy(out=part_of(mean, before), in_=sums_of("y", before))
+        nc.scalar.activation(out=part_of(mean_sq, before), in_=sums_of("y", before), func=ACT.Square)
+        head_sums(ahead[-1])
+        for j in ahead:
+            fold("spread", j)
         add_b3(last)
         head_functions(last)
         fold("y", last)
-        for j in (before, last):
+        for j in ends:
             head_sums(j)
             fold("spread", j)
             nc.scalar.activation(out=part_of(log_sum, j), in_=part_of(factors, j), func=ACT.Ln)
-        n = tiles_of(parts[last][1])[1]
-        nc.vector.tensor_copy(out=part_of(mean, last), in_=held["y", "sums", parts[last][1]][:, 0:n, :])
+        nc.vector.tensor_copy(out=part_of(mean, last), in_=sums_of("y", last))
         nc.sync.dma_start(out=out_0.rearrange("(p i) o -> p i o", i=TILES), in_=mean[:])
-        nc.vector.tensor_tensor(out=part_of(mean_sq, last), in0=part_of(mean, last), in1=part_of(mean, last), op=ALU.mult)
-        for j in (before, last):
-            n = tiles_of(parts[j][1])[1]
+        nc.vector.tensor_tensor(
+            out=part_of(mean_sq, last), in0=part_of(mean, last), in1=part_of(mean, last), op=ALU.mult
+        )
+        for j in ends:
             nc.vector.tensor_tensor(
-                out=part_of(variance, j),
-                in0=held["spread", "sums", parts[j][1]][:, 0:n, :],
-                in1=part_of(mean_sq, j),
-                op=ALU.subtract,
+                out=part_of(variance, j), in0=sums_of("spread", j), in1=part_of(mean_sq, j), op=ALU.subtract
             )
-        for j in (before, last):
+        for j in ends:
             nc.vector.scalar_tensor_tensor(
-                out=part_of(variance, j), in0=part_of(log_sum, j), scalar=1.0 / MODELS, in1=part_of(variance, j), op0=ALU.mult, op1=ALU.add
+                out=part_of(variance, j),
+                in0=part_of(log_sum, j),
+                scalar=1.0 / MODELS,
+                in1=part_of(variance, j),
+                op0=ALU.mult,
+                op1=ALU.add,
             )
-        for j in (before, last):
-            lo, n = tiles_of(parts[j][1])
+        for j in ends:
             nc.vector.tensor_scalar(
-                out=part_of(variance, j), in0=part_of(variance, j), scalar1=0.0, scalar2=EPS, op0=ALU.max, op1=ALU.add
+                out=part_of(variance, j),
+                in0=part_of(variance, j),
+                scalar1=0.0,
+                scalar2=EPS,
+                op0=ALU.max,
+                op1=ALU.add,
             )
             nc.sync.dma_start(
-                out=out_1.rearrange("(p i) o -> p i o", i=TILES)[:, lo : lo + n, :], in_=part_of(variance, j)
+                out=part_of(out_1.rearrange("(p i) o -> p i o", i=TILES), j), in_=part_of(variance, j)
             )

import math
from contextlib import ExitStack

import concourse.mybir as mybir
from concourse.masks import make_identity

F32 = mybir.dt.float32
BF16 = mybir.dt.bfloat16
I32 = mybir.dt.int32
U32 = mybir.dt.uint32
U8 = mybir.dt.uint8
FP8X4 = mybir.dt.float8_e4m3fn_x4
ALU = mybir.AluOpType
ACT = mybir.ActivationFunctionType

MODELS = 5
BATCH = 896
HIDDEN = 1024
OUT2 = 128
OUT = OUT2 // 2
EPS = 1e-6

P = 128
PACK = 4
K_PASS = P * PACK
PASSES = HIDDEN // K_PASS
TILES = BATCH // P
BANK = 512
PLANES = 4

SLICES = ((0, 4), (4, 2), (6, 1))
H1_BUFS = 3
W2_BUFS = 3

FOLD_FROM = MODELS - 2
FLIP_BANKS = 3
AHEAD = 2

FLOPS = 2 * MODELS * BATCH * HIDDEN * (HIDDEN + OUT2)


def parts_of_the_batch():
    return [(m, slices) for m in range(MODELS) for slices in ((0,), (1, 2))]


def tiles_of(slices):
    return SLICES[slices[0]][0], sum(SLICES[s][1] for s in slices)


def tile_gaussianmixturemlp_pa_t_e_kernel(
    tc, h1, W2_words, W2_scales, b2, W3_words, W3_scales, b3, out_0, out_1
):
    nc = tc.nc
    all_passes = MODELS * PASSES
    plane_tiles = (all_passes + PLANES - 1) // PLANES
    parts = parts_of_the_batch()
    n_units = PASSES * len(parts)
    first_unit = [min(PASSES * j for j in range(len(parts)) if parts[j][0] == m) for m in range(MODELS)]
    last_part = [max(j for j in range(len(parts)) if parts[j][0] == m) for m in range(MODELS)]
    last = len(parts) - 1

    with ExitStack() as ctx:
        keep = ctx.enter_context(tc.tile_pool(name="keep", bufs=1))
        stage = ctx.enter_context(tc.tile_pool(name="stage", bufs=2))
        psum_flip = ctx.enter_context(tc.psum_pool(name="psum_flip", bufs=FLIP_BANKS))
        psum_h2 = ctx.enter_context(tc.psum_pool(name="psum_h2", bufs=4))
        psum_y = ctx.enter_context(tc.psum_pool(name="psum_y", bufs=1))
        ctx.enter_context(tc.manual_schedule())

        w2_sorted = keep.tile([P, all_passes, PACK * HIDDEN], U8, align_bytes=64)
        w3_words = keep.tile([P, all_passes, PACK * OUT2], U8, align_bytes=64)
        w2_planes = keep.tile([P, plane_tiles, HIDDEN], U8, align_bytes=64)
        w2_planes_sorted = keep.tile([P, plane_tiles, HIDDEN], U8, align_bytes=64)
        w3_planes = keep.tile([P, all_passes, OUT2], U8, align_bytes=64)
        b2_bf = keep.tile([P, MODELS * PASSES, PACK], BF16)
        b2_cols = keep.tile([P, MODELS * PASSES, PACK], F32)
        b3_all = keep.tile([P, MODELS, OUT2], BF16)
        ident = keep.tile([P, P], F32)
        fifth = keep.tile([P, P], F32)
        var_sum = keep.tile([P, TILES, OUT], F32)
        mean_sum = keep.tile([P, TILES, OUT], F32)
        factors = keep.tile([P, TILES, OUT], F32)
        mean = keep.tile([P, TILES, OUT], F32)
        mean_sq = keep.tile([P, TILES, OUT], F32)
        variance = keep.tile([P, TILES, OUT], F32)

        nc.vector.memset(w2_planes[:].bitcast(I32), 0)
        nc.vector.memset(w3_planes[:].bitcast(I32), 0)
        make_identity(nc, ident[:])
        nc.vector.tensor_scalar_mul(out=fifth[:], in0=ident[:], scalar1=1.0 / MODELS)

        held = {}

        def load_h1(m, first, count):
            if ("h1_rows", m) not in held:
                h1_new = stage.tile([P, TILES, HIDDEN], BF16, tag="h1_rows", bufs=H1_BUFS)
                held["h1_rows", m] = h1_new
            rows = h1[m].rearrange("(p i) k -> p i k", i=TILES)
            nc.sync.dma_start(
                out=held["h1_rows", m][:, first : first + count, :], in_=rows[:, first : first + count, :]
            )

        def load_w2(m, G):
            w2_new = stage.tile([P, PASSES, PACK * BANK], U8, tag="w2_raw%d" % G, bufs=W2_BUFS)
            held["w2_raw", m, G] = w2_new
            c0 = PASSES * m
            some = slice(PACK * BANK * G, PACK * BANK * (G + 1))
            nc.sync.dma_start(
                out=w2_new[:].bitcast(I32),
                in_=W2_words[c0 : c0 + PASSES].rearrange("g p n t -> p g (n t)")[:, :, some].bitcast(I32),
            )

        def load_w2_planes(c0):
            n_planes = min(PLANES, all_passes - c0)
            for quadrant in range(4):
                nc.sync.dma_start(
                    out=w2_planes[:].bitcast(I32)[
                        32 * quadrant : 32 * quadrant + 4 * n_planes, c0 // PLANES, :
                    ],
                    in_=W2_scales[c0 : c0 + n_planes, 4 * quadrant : 4 * quadrant + 4, :].bitcast(I32),
                )

        def load_w3_planes():
            for quadrant in range(4):
                nc.sync.dma_start(
                    out=w3_planes[:].bitcast(I32)[32 * quadrant : 32 * quadrant + 4, :, :],
                    in_=W3_scales[:, 4 * quadrant : 4 * quadrant + 4, :]
                    .rearrange("c r n -> r c n")
                    .bitcast(I32),
                )

        def load_w3(c0, c1):
            nc.sync.dma_start(
                out=w3_words[:, c0:c1, :].bitcast(I32),
                in_=W3_words[c0:c1].rearrange("g p n t -> p g (n t)").bitcast(I32),
            )

        def load_b3():
            nc.sync.dma_start(
                out=b3_all[:].rearrange("p m o -> p (m o)"),
                in_=b3.rearrange("m o -> (m o)").partition_broadcast(P),
            )

        def load_b2():
            nc.sync.dma_start(
                out=b2_bf[:], in_=b2.rearrange("m (g p t) -> p (m g) t", g=PASSES, t=PACK)
            )

        load_h1(0, 0, 1)
        load_h1(0, 1, 1)
        load_w2_planes(0)
        load_h1(0, 2, 2)
        load_h1(0, 4, 2)
        load_w2(0, 0)
        load_h1(0, 6, 1)
        load_b2()
        load_w2(0, 1)
        load_h1(1, 0, 2)
        load_h1(1, 2, 2)
        load_w2(1, 0)
        load_h1(1, 4, 3)
        load_w2(1, 1)
        load_w3_planes()
        load_w3(0, PASSES)
        load_b3()
        load_h1(2, 0, 4)
        load_w3(PASSES, all_passes)
        load_w2_planes(PLANES)
        load_w2_planes(2 * PLANES)
        load_h1(2, 4, 3)
        load_w2(2, 0)
        load_w2(2, 1)

        def sort_w2(m, G):
            c0 = PASSES * m
            some = slice(PACK * BANK * G, PACK * BANK * (G + 1))
            nc.vector.tensor_copy(
                out=w2_sorted[:, c0 : c0 + PASSES, some].bitcast(I32).rearrange("p c (t i) -> p c i t", t=PACK),
                in_=held["w2_raw", m, G][:].bitcast(I32).rearrange("p c (i t) -> p c i t", t=PACK),
            )
            if m + W2_BUFS < MODELS:
                load_w2(m + W2_BUFS, G)

        def sort_w2_planes(tile_no):
            nc.vector.tensor_copy(
                out=w2_planes_sorted[:, tile_no, :].rearrange("p (g t i) -> p g t i", g=PASSES, t=PACK),
                in_=w2_planes[:, tile_no, :].rearrange("p (g i t) -> p g t i", g=PASSES, t=PACK),
            )

        def rows_behind(k):
            j, half = divmod(k, PASSES)
            if not 0 <= j + AHEAD < len(parts):
                return []
            m, slices = parts[j + AHEAD]
            mine = [(m, s, i) for s in slices for i in range(SLICES[s][1])]
            cut = len(mine) if len(mine) <= FLIP_BANKS else (len(mine) + 1) // 2
            return mine[:cut] if half == 0 else mine[cut:]

        def words_of(m, s, i):
            return held["h1_rows", m][:].bitcast(F32)[:, SLICES[s][0] + i, :]

        def split_words(k):
            if k % PASSES == 0:
                for m, s, i in rows_behind(k)[:2]:
                    if m == 2 or (m == 1 and s > 0):
                        split_new = stage.tile([P, PASSES, 2, P], F32, tag="h1_split", bufs=4)
                        nc.vector.tensor_copy(
                            out=split_new[:],
                            in_=words_of(m, s, i).rearrange("p (g w u) -> p g u w", g=PASSES, u=2),
                        )
                        held["h1_split", m, s, i] = split_new

        def transpose_h1(k):
            rows = rows_behind(k)
            for m, s, i in rows:
                if i == 0:
                    grouped_new = stage.tile(
                        [P, PASSES, SLICES[s][1], P, PACK], BF16, tag="h1_grouped%d" % s, bufs=1, align_bytes=64
                    )
                    held["h1_grouped", m, s] = grouped_new
                flipped = psum_flip.tile([P, PASSES * 2, P], F32, tag="flipped")
                for g in range(PASSES):
                    for u in range(2):
                        if ("h1_split", m, s, i) in held:
                            words = held["h1_split", m, s, i][:, g, u, :]
                        else:
                            words = words_of(m, s, i)[:, 2 * P * g + u : 2 * P * (g + 1) : 2]
                        nc.tensor.transpose(flipped[:, 2 * g + u, :], words, ident[:])
                copy = nc.vector.tensor_copy if k % PASSES == 1 and (m, s, i) == rows[0] else nc.scalar.copy
                copy(
                    out=held["h1_grouped", m, s][:, :, i].bitcast(F32),
                    in_=flipped[:].rearrange("p (g u) b -> p g b u", u=2),
                )
            j = k // PASSES + AHEAD
            if k % PASSES == 1 and j in last_part and parts[j][0] + H1_BUFS < MODELS:
                load_h1(parts[j][0] + H1_BUFS, 0, TILES)

        def quantise_h1(j, half=None):
            m, slices = parts[j]
            for s in slices:
                count = SLICES[s][1]
                grouped = held["h1_grouped", m, s]
                if half != 1:
                    codes_new = stage.tile([P, PASSES, count * P], U32, tag="h1_codes%d" % s, align_bytes=64)
                    scales_new = stage.tile([P, PASSES, count * P], U8, tag="h1_scales%d" % s, align_bytes=64)
                    held["h1_mx", m, s] = (codes_new, scales_new)
                codes, scales = held["h1_mx", m, s]
                if half is None:
                    nc.vector.quantize_mx(
                        out=codes[:].rearrange("p g c -> p (g c)").bitcast(FP8X4),
                        scales=scales[:].rearrange("p g c -> p (g c)"),
                        in_=grouped[:].rearrange("p g i b t -> p (g i b t)"),
                    )
                    continue
                lo, hi = half * count // 2, (half + 1) * count // 2
                for g in range(PASSES):
                    nc.vector.quantize_mx(
                        out=codes[:, g, P * lo : P * hi].bitcast(FP8X4),
                        scales=scales[:, g, P * lo : P * hi],
                        in_=grouped[:, g, lo:hi].rearrange("p i b t -> p (i b t)"),
                    )

        def layer2(k):
            j, G = divmod(k, PASSES)
            m, slices = parts[j]
            width = P * tiles_of(slices)[1]
            h2_rows = stage.tile([P, PACK, BANK], BF16, tag="h2_rows", bufs=3)
            for t in range(PACK):
                col = P * (PACK * G + t)
                bank = psum_h2.tile([P, BANK], F32, tag="h2_bank")
                at = 0
                for s in slices:
                    n = P * SLICES[s][1]
                    codes, scales = held["h1_mx", m, s]
                    for g in range(PASSES):
                        c = PASSES * m + g
                        nc.tensor.matmul_mx(
                            out=bank[:, at : at + n],
                            lhsT=w2_sorted[:, c, PACK * col : PACK * (col + P)].bitcast(FP8X4),
                            lhsT_scale=w2_planes_sorted[4 * (c % PLANES) : P, c // PLANES, col : col + P],
                            rhs=codes[:, g, :].bitcast(FP8X4),
                            rhs_scale=scales[:, g, :],
                            start=(g == 0),
                            stop=(g == PASSES - 1),
                        )
                    at += n
                nc.scalar.activation(
                    out=h2_rows[:, t, 0:width],
                    in_=bank[:, 0:width],
                    func=ACT.Relu,
                    bias=b2_cols[:, PASSES * m + G, t : t + 1],
                )
            held["h2_rows", k] = h2_rows

        def interleave_h2(k):
            j, G = divmod(k, PASSES)
            width = P * tiles_of(parts[j][1])[1]
            if G == 0:
                new_grouped = stage.tile([P, PASSES, width, PACK], BF16, tag="h2_grouped", align_bytes=64)
                held["h2_grouped", j] = new_grouped
            nc.vector.tensor_copy(
                out=held["h2_grouped", j][:, G].rearrange("p (c i) t -> p c t i", i=4),
                in_=held["h2_rows", k][:, :, 0:width].rearrange("p t (c i) -> p c t i", i=4),
            )

        def quantise_h2(j):
            columns = PASSES * P * tiles_of(parts[j][1])[1]
            codes = stage.tile([P, columns], U32, tag="h2_codes", align_bytes=64)
            scales = stage.tile([P, columns], U8, tag="h2_scales", align_bytes=64)
            flat = held["h2_grouped", j][:].rearrange("p g n t -> p (g n t)")
            lo = 0
            while lo < columns:
                hi = lo + max(w for w in (128, 256, 512, 1024) if w <= columns - lo)
                nc.vector.quantize_mx(
                    out=codes[:, lo:hi].bitcast(FP8X4),
                    scales=scales[:, lo:hi],
                    in_=flat[:, PACK * lo : PACK * hi],
                )
                lo = hi
            held["h2_mx", j] = (codes, scales)

        def layer3(j):
            m, slices = parts[j]
            count = tiles_of(slices)[1]
            codes, scales = held["h2_mx", j]
            y_bank = psum_y.tile([P, BANK // OUT2, OUT2], F32, tag="y_bank")
            for i in range(count):
                for G in range(PASSES):
                    c = PASSES * m + G
                    cols = slice(P * (count * G + i), P * (count * G + i + 1))
                    nc.tensor.matmul_mx(
                        out=y_bank[:, i, :],
                        lhsT=codes[:, cols].bitcast(FP8X4),
                        lhsT_scale=scales[:, cols],
                        rhs=w3_words[:, c, :].bitcast(FP8X4),
                        rhs_scale=w3_planes[:, c, :],
                        start=(G == 0),
                        stop=(G == PASSES - 1),
                    )
            held["y_bank", j] = y_bank

        def add_b3(j):
            m, slices = parts[j]
            n = tiles_of(slices)[1]
            y = stage.tile([P, BANK // OUT2, OUT2], F32, tag="y", bufs=5)
            held["y", j] = y
            nc.vector.tensor_tensor(
                out=y[:, 0:n, :],
                in0=held["y_bank", j][:, 0:n, :],
                in1=b3_all[:, m, :].unsqueeze(1).to_broadcast([P, n, OUT2]),
                op=ALU.add,
            )

        def head_functions(j):
            n = tiles_of(parts[j][1])[1]
            y = held["y", j]
            size = stage.tile([P, BANK // OUT2, OUT], F32, tag="size", bufs=2)
            square = stage.tile([P, BANK // OUT2, OUT], F32, tag="square", bufs=3)
            decay = stage.tile([P, BANK // OUT2, OUT], F32, tag="decay", bufs=3)
            nc.scalar.activation(out=size[:, 0:n, :], in_=y[:, 0:n, OUT:OUT2], func=ACT.Abs)
            nc.scalar.activation(out=square[:, 0:n, :], in_=y[:, 0:n, 0:OUT], func=ACT.Square)
            nc.scalar.activation(out=decay[:, 0:n, :], in_=size[:, 0:n, :], func=ACT.Exp, scale=-1.0)
            held["functions", j] = (square, decay)

        def part_of(tile, j):
            lo, n = tiles_of(parts[j][1])
            return tile[:, lo : lo + n, :]

        def head_sums(j):
            m, slices = parts[j]
            n = tiles_of(slices)[1]
            means = held["y", j][:, 0:n, 0:OUT]
            raw = held["y", j][:, 0:n, OUT:OUT2]
            square, decay = [tile[:, 0:n, :] for tile in held["functions", j]]
            if m == 0:
                nc.vector.tensor_scalar(
                    out=part_of(factors, j),
                    in0=decay,
                    scalar1=1.0,
                    scalar2=math.exp(MODELS * EPS),
                    op0=ALU.add,
                    op1=ALU.mult,
                )
                nc.vector.tensor_copy(out=part_of(mean_sum, j), in_=means)
                nc.vector.scalar_tensor_tensor(
                    out=part_of(var_sum, j), in0=raw, scalar=0.0, in1=square, op0=ALU.max, op1=ALU.add
                )
                return
            nc.vector.scalar_tensor_tensor(
                out=part_of(factors, j), in0=decay, scalar=1.0, in1=part_of(factors, j), op0=ALU.add, op1=ALU.mult
            )
            if m >= FOLD_FROM:
                spread = stage.tile([P, BANK // OUT2, OUT], F32, tag="spread", bufs=4)
                held["spread", j] = spread
                nc.vector.scalar_tensor_tensor(
                    out=spread[:, 0:n, :], in0=raw, scalar=0.0, in1=square, op0=ALU.max, op1=ALU.add
                )
                return
            nc.vector.scalar_tensor_tensor(
                out=part_of(var_sum, j), in0=raw, scalar=0.0, in1=part_of(var_sum, j), op0=ALU.max, op1=ALU.add
            )
            nc.vector.tensor_tensor(out=part_of(mean_sum, j), in0=part_of(mean_sum, j), in1=means, op=ALU.add)
            nc.vector.tensor_tensor(out=part_of(var_sum, j), in0=part_of(var_sum, j), in1=square, op=ALU.add)

        def sums_of(what, j):
            return held[what, "sums", parts[j][1]][:, 0 : tiles_of(parts[j][1])[1], :]

        def fold(what, j):
            m, slices = parts[j]
            n = tiles_of(slices)[1]
            if m == FOLD_FROM:
                if what == "spread" and slices[0] > 0:
                    pool, tag = psum_h2, "h2_bank"
                else:
                    pool, tag = psum_flip, "flipped"
                sums_new = pool.tile([P, BANK // OUT, OUT], F32, tag=tag)
                held[what, "sums", slices] = sums_new
                first_models = mean_sum if what == "y" else var_sum
                nc.tensor.matmul(
                    sums_of(what, j), lhsT=fifth[:], rhs=part_of(first_models, j), start=True, stop=False
                )
            nc.tensor.matmul(
                sums_of(what, j),
                lhsT=fifth[:],
                rhs=held[what, j][:, 0:n, 0:OUT],
                start=False,
                stop=(m == MODELS - 1),
            )

        def part(stage_of_part, j):
            if 0 <= j < len(parts):
                stage_of_part(j)

        def unit(stage_of_unit, k):
            if 0 <= k < n_units:
                stage_of_unit(k)

        before = last - 1
        ahead = [j for j in range(before) if parts[j][0] == MODELS - 2]
        sort_w2_planes(0)
        for k in range(-PASSES * AHEAD, n_units + PASSES):
            j, G = divmod(k, PASSES)
            if G == 1:
                part(add_b3, j - 2)
                part(quantise_h2, j - 1)
            unit(interleave_h2, k - 1)
            if G == 1:
                part(head_sums, j - 4)
            for m in range(1, MODELS):
                if k == first_unit[m] - 5 and (PASSES * m) % PLANES == 0:
                    sort_w2_planes(PASSES * m // PLANES)
                if k == first_unit[m] - 3:
                    sort_w2(m, 0)
                if k == first_unit[m] - 1:
                    sort_w2(m, 1)
            if k == -3:
                quantise_h1(0, 0)
            if k == -2:
                sort_w2(0, 0)
                quantise_h1(0, 1)
            if k == -1:
                nc.vector.tensor_copy(out=b2_cols[:], in_=b2_bf[:])
                sort_w2(0, 1)
            if G == 0:
                if j >= 0:
                    part(quantise_h1, j + 1)
                part(layer3, j - 2)
            split_words(k + 1)
            unit(layer2, k)
            transpose_h1(k)
            if G == 1:
                part(head_functions, j - 3)
            if k == n_units:
                for j in ahead:
                    fold("y", j)

        log_sum = keep.tile([P, TILES, OUT], F32)
        ends = (before, last)
        fold("y", before)
        layer3(last)
        head_functions(before)
        nc.scalar.copy(out=part_of(mean, before), in_=sums_of("y", before))
        nc.scalar.activation(out=part_of(mean_sq, before), in_=sums_of("y", before), func=ACT.Square)
        head_sums(ahead[-1])
        for j in ahead:
            fold("spread", j)
        add_b3(last)
        head_functions(last)
        fold("y", last)
        for j in ends:
            head_sums(j)
            fold("spread", j)
            nc.scalar.activation(out=part_of(log_sum, j), in_=part_of(factors, j), func=ACT.Ln)
        nc.vector.tensor_copy(out=part_of(mean, last), in_=sums_of("y", last))
        nc.sync.dma_start(out=out_0.rearrange("(p i) o -> p i o", i=TILES), in_=mean[:])
        nc.vector.tensor_tensor(
            out=part_of(mean_sq, last), in0=part_of(mean, last), in1=part_of(mean, last), op=ALU.mult
        )
        for j in ends:
            nc.vector.tensor_tensor(
                out=part_of(variance, j), in0=sums_of("spread", j), in1=part_of(mean_sq, j), op=ALU.subtract
            )
        for j in ends:
            nc.vector.scalar_tensor_tensor(
                out=part_of(variance, j),
                in0=part_of(log_sum, j),
                scalar=1.0 / MODELS,
                in1=part_of(variance, j),
                op0=ALU.mult,
                op1=ALU.add,
            )
        for j in ends:
            nc.vector.tensor_scalar(
                out=part_of(variance, j),
                in0=part_of(variance, j),
                scalar1=0.0,
                scalar2=EPS,
                op0=ALU.max,
                op1=ALU.add,
            )
            nc.sync.dma_start(
                out=part_of(out_1.rearrange("(p i) o -> p i o", i=TILES), j), in_=part_of(variance, j)
            )
